import numpy as np
import ml_dtypes


def mxq(x, axis, fmt="e4m3"):
    dtype, down = {"e4m3": (ml_dtypes.float8_e4m3fn, 7), "e5m2": (ml_dtypes.float8_e5m2, 14)}[fmt]
    v = np.moveaxis(np.asarray(x, np.float32).astype(ml_dtypes.bfloat16).astype(np.float64), axis, -1)
    blocks = v.reshape(v.shape[:-1] + (-1, 32))
    amax = np.abs(blocks).max(-1, keepdims=True)
    byte = np.maximum(np.where(amax > 0, np.frexp(amax)[1] - 1 + 127, 0) - down, 1)
    scale = np.exp2(byte - 127.0)
    codes = (blocks / scale).astype(np.float32).astype(dtype).astype(np.float64)
    return np.moveaxis((codes * scale).reshape(v.shape), -1, axis)


WIDE = False


def mx_kscale(k):
    if not WIDE:
        return np.ones(k)
    levels = np.array([10, -10, 5, -5, 0])
    a = np.random.permutation(np.resize(levels, k // 512 * 4)).reshape(k // 512, 4)
    idx = np.arange(k)
    return np.exp2(a[idx // 512, idx % 128 // 32])


BF16 = ml_dtypes.bfloat16


def bf(x):
    return np.asarray(x, np.float32).astype(BF16)


def f64(x):
    return np.asarray(x).astype(np.float64)


B, S, E, H, KV, HD, HID = 2, 2048, 512, 4, 2, 128, 3072
F = (H + 2 * KV) * HD
EPS = 1e-6
ROPE_BASE = 1000000.0


def rmsnorm(v, w):
    var = np.mean(v * v, axis=-1, keepdims=True)
    return v * (1.0 / np.sqrt(var + EPS)) * w


def apply_rope(v, cos, sin):
    v1 = v[..., 0::2]
    v2 = v[..., 1::2]
    r1 = v1 * cos - v2 * sin
    r2 = v1 * sin + v2 * cos
    return np.stack([r1, r2], axis=-1).reshape(v.shape)


def setup_inputs():
    s = mx_kscale(E)
    return {"x": bf(np.random.standard_normal((B, S, E)) * 2.0),
            "ln_w": bf((1.0 + 0.1 * np.random.standard_normal(E)) * s),
            "qkv_w": bf(np.random.standard_normal((E, F)) * 2.0 / np.sqrt(E) / s[:, None]),
            "q_norm_w": bf(1.0 + 0.1 * np.random.standard_normal(HD)),
            "k_norm_w": bf(1.0 + 0.1 * np.random.standard_normal(HD))}


def reference(x, ln_w, qkv_w, q_norm_w, k_norm_w):
    h = rmsnorm(f64(x), f64(ln_w))
    qkv = mxq(h, 2, "e4m3") @ mxq(f64(qkv_w), 0, "e4m3")
    q = qkv[..., : H * HD].reshape(B, S, H, HD)
    k = qkv[..., H * HD : (H + KV) * HD].reshape(B, S, KV, HD)
    v = qkv[..., (H + KV) * HD :].reshape(B, S, KV, HD)
    q = rmsnorm(q, f64(q_norm_w))
    k = rmsnorm(k, f64(k_norm_w))
    pos = np.arange(S, dtype=np.float64)
    inv_freq = 1.0 / (ROPE_BASE ** (np.arange(0, HD, 2, dtype=np.float64) / HD))
    ang = pos[:, None] * inv_freq
    cos = np.cos(ang)[None, :, None, :]
    sin = np.sin(ang)[None, :, None, :]
    return apply_rope(q, cos, sin), apply_rope(k, cos, sin), v

@@ -1,0 +1,284 @@
+import math
+from contextlib import ExitStack
+
+import concourse.mybir as mybir
+from concourse.masks import make_identity
+
+FLOPS = 2 * 4096 * 512 * 1024
+
+F32 = mybir.dt.float32
+BF16 = mybir.dt.bfloat16
+I32 = mybir.dt.int32
+U32 = mybir.dt.uint32
+U8 = mybir.dt.uint8
+FP8X4 = mybir.dt.float8_e4m3fn_x4
+ALU = mybir.AluOpType
+ACT = mybir.ActivationFunctionType
+
+P = 128
+NB = 2
+E = 512
+A = 16
+NH = 6
+HD = 128
+HALF = 64
+EPS = 1e-6
+NT = NB * A
+
+
+def tile_qwen3block_pa_t_kernel(tc, x, ln_w, qkv_w, q_norm_w, k_norm_w, out_0, out_1, out_2):
+    nc = tc.nc
+    with ExitStack() as ctx:
+        const = ctx.enter_context(tc.tile_pool(name="const", bufs=1))
+        small = ctx.enter_context(tc.tile_pool(name="small", bufs=4))
+        xs_pool = ctx.enter_context(tc.tile_pool(name="xs_pool", bufs=3))
+        h_pool = ctx.enter_context(tc.tile_pool(name="h_pool", bufs=3))
+        t_pool = ctx.enter_context(tc.tile_pool(name="t_pool", bufs=3))
+        o_pool = ctx.enter_context(tc.tile_pool(name="o_pool", bufs=3))
+        ps_t = ctx.enter_context(tc.psum_pool(name="ps_t", bufs=2))
+        ps_mx = ctx.enter_context(tc.psum_pool(name="ps_mx", bufs=3))
+
+        xv = x.rearrange("b (p a) e -> b p a e", a=A)
+        o0v = out_0.rearrange("b (p a) h d -> b p a (h d)", a=A)
+        o1v = out_1.rearrange("b (p a) h d -> b p a (h d)", a=A)
+        o2v = out_2.rearrange("b (p a) h d -> b p a (h d)", a=A)
+
+        def tile_coords(i):
+            g = i // 2
+            return g // 2, g % 2, i % 2
+
+        l0 = const.tile([P, P], BF16)
+        nc.vector.memset(l0[:], 0.0)
+        nc.scalar.dma_start(out=l0[0:4, :], in_=ln_w.rearrange("(t c) -> t c", c=P))
+        wn = const.tile([P, 2, HD], BF16)
+        nc.scalar.dma_start(out=wn[:, 0, :], in_=q_norm_w.partition_broadcast(P))
+        nc.scalar.dma_start(out=wn[:, 1, :], in_=k_norm_w.partition_broadcast(P))
+
+        xin = {}
+        wr = const.tile([P, 4, 1024], BF16)
+        for g in range(NT // 2):
+            ap, b = g // 2, g % 2
+            xg = const.tile([P, 2, E], BF16, name="xg%d" % g)
+            nc.sync.dma_start(out=xg[:], in_=xv[b, :, 2 * ap : 2 * ap + 2, :])
+            xin[g] = xg
+            if g == 0:
+                nc.sync.dma_start(out=wr[:], in_=qkv_w.rearrange("(t p) n -> p t n", p=P))
+
+        pos_i = const.tile([P, A], I32)
+        nc.gpsimd.iota(pos_i[:], pattern=[[1, A]], base=0, channel_multiplier=A)
+        identf = const.tile([P, P], F32)
+        make_identity(nc, identf[:])
+
+        one1 = const.tile([P, 1], F32)
+        nc.vector.memset(one1[:], 1.0)
+        eps_t = const.tile([P, 1], F32)
+        nc.vector.memset(eps_t[:], EPS)
+        gt = const.tile([P, HALF], F32)
+        nc.vector.tensor_scalar_mul(out=gt[:, 0:1], in0=one1[:], scalar1=1.0 / (2.0 * math.pi))
+        n = 1
+        while n < HALF:
+            nc.vector.tensor_scalar_mul(out=gt[:, n : 2 * n], in0=gt[:, 0:n], scalar1=1000000.0 ** (-n / 64.0))
+            n *= 2
+        pos_f = const.tile([P, A], F32)
+        nc.vector.tensor_copy(out=pos_f[:], in_=pos_i[:])
+
+        tt = const.tile([P, A, HALF], F32)
+        n_s = const.tile([P, A, HALF], I32)
+        f_s = const.tile([P, A, HALF], F32)
+        n_c = const.tile([P, A, HALF], I32)
+        f_c = const.tile([P, A, HALF], F32)
+        sin_t = const.tile([P, A, HALF], F32)
+        cos_t = const.tile([P, A, HALF], F32)
+        for a0, a1 in ((0, 8), (8, 16)):
+            na = a1 - a0
+            nc.vector.tensor_tensor(
+                out=tt[:, a0:a1, :],
+                in0=pos_f[:, a0:a1].unsqueeze(2).to_broadcast([P, na, HALF]),
+                in1=gt[:].unsqueeze(1).to_broadcast([P, na, HALF]),
+                op=ALU.mult,
+            )
+            nc.vector.tensor_copy(out=n_s[:, a0:a1, :], in_=tt[:, a0:a1, :])
+            nc.vector.tensor_scalar_add(out=n_c[:, a0:a1, :], in0=tt[:, a0:a1, :], scalar1=0.25)
+            nc.vector.tensor_tensor(out=f_s[:, a0:a1, :], in0=tt[:, a0:a1, :], in1=n_s[:, a0:a1, :], op=ALU.subtract)
+            nc.vector.scalar_tensor_tensor(
+                out=f_c[:, a0:a1, :], in0=tt[:, a0:a1, :], scalar=0.25, in1=n_c[:, a0:a1, :],
+                op0=ALU.add, op1=ALU.subtract,
+            )
+            nc.scalar.activation(out=sin_t[:, a0:a1, :], in_=f_s[:, a0:a1, :], func=ACT.Sin, scale=2.0 * math.pi)
+            nc.scalar.activation(out=cos_t[:, a0:a1, :], in_=f_c[:, a0:a1, :], func=ACT.Sin, scale=2.0 * math.pi)
+
+        wd = const.tile([P, 2, 3, HALF], F32)
+        nc.vector.tensor_copy(out=wd[:, :, 0:2, :], in_=wn[:].rearrange("p q (j e) -> p q e j", e=2))
+        nc.vector.tensor_scalar_mul(out=wd[:, :, 2, :], in0=wd[:, :, 1, :], scalar1=-1.0)
+
+        l0f = const.tile([P, P], F32)
+        nc.vector.tensor_copy(out=l0f[:], in_=l0[:])
+        xT = ps_t.tile([P, 4, P], F32)
+        nc.tensor.transpose(out=xT[:, 0, :], in_=l0f[:], identity=identf[:])
+        lnw4 = const.tile([P, 4], F32)
+        nc.vector.tensor_copy(out=lnw4[:], in_=xT[:, 0, 0:4])
+
+        wg = const.tile([P, 1024, 4], BF16, align_bytes=64)
+        wc = const.tile([P, 1024], U32, align_bytes=64)
+        ws = const.tile([P, 1024], U8, align_bytes=64)
+        wg_qk = wg[:, 0:768, :].rearrange("p (h e j) t -> p e h j t", e=2, j=HALF)
+        wr_qk = wr[:, :, 0:768].rearrange("p t (h j e) -> p e h j t", e=2, j=HALF)
+        for e in range(2):
+            nc.gpsimd.tensor_scalar(
+                out=wg_qk[:, e, 0:4, :, :], in0=wr_qk[:, e, 0:4, :, :], scalar1=1.0, scalar2=0.0, op0=ALU.mult, op1=ALU.add
+            )
+        for e in range(2):
+            nc.vector.tensor_copy(out=wg_qk[:, e, 4:6, :, :], in_=wr_qk[:, e, 4:6, :, :])
+        nc.vector.tensor_copy(out=wg[:, 768:1024, :], in_=wr[:, :, 768:1024].rearrange("p t n -> p n t"))
+        for c in range(2):
+            nc.vector.quantize_mx(
+                out=wc[:, 512 * c : 512 * c + 512].bitcast(FP8X4),
+                scales=ws[:, 512 * c : 512 * c + 512],
+                in_=wg[:, 512 * c : 512 * c + 512, :].rearrange("p n t -> p (n t)"),
+            )
+
+        tab = const.tile([P, A, 2, 2, HD], F32)
+
+        def build_tables(eng, a0, a1):
+            na = a1 - a0
+            for qk in range(2):
+                for e_out, hf, src, slot in ((0, 0, cos_t, 0), (0, 1, sin_t, 2), (1, 0, sin_t, 0), (1, 1, cos_t, 1)):
+                    eng.tensor_tensor(
+                        out=tab[:, a0:a1, qk, e_out, HALF * hf : HALF * hf + HALF],
+                        in0=src[:, a0:a1, :],
+                        in1=wd[:, qk, slot, :].unsqueeze(1).to_broadcast([P, na, HALF]),
+                        op=ALU.mult,
+                    )
+
+        build_tables(nc.vector, 0, 2)
+        build_tables(nc.gpsimd, 2, 8)
+
+        ssx = const.tile([P, NT], F32)
+        rx = const.tile([P, NT], F32)
+        junk_x = const.tile([P, E], BF16)
+        junk_h = const.tile([P, HD], BF16)
+        st = {}
+
+        def stage_a(i):
+            xt = xin[i // 2][:, i % 2, :]
+            nc.scalar.activation(out=junk_x[:], in_=xt, func=ACT.Square, accum_out=ssx[:, i : i + 1])
+            nc.scalar.activation(
+                out=rx[:, i : i + 1], in_=ssx[:, i : i + 1], func=ACT.Abs_reciprocal_sqrt,
+                scale=1.0 / E, bias=eps_t[:],
+            )
+
+        def stage_b(i):
+            xt = xin[i // 2][:, i % 2, :]
+            xs = xs_pool.tile([P, E], F32)
+            if i % 2 == 1:
+                nc.scalar.activation(out=xs[:], in_=xt, func=ACT.Copy, scale=rx[:, i : i + 1])
+            else:
+                nc.gpsimd.tensor_scalar(
+                    out=xs[:], in0=xt, scalar1=rx[:, i : i + 1], scalar2=0.0, op0=ALU.mult, op1=ALU.add
+                )
+            st[("xs", i)] = xs
+
+        def stage_c(i):
+            xs = st[("xs", i)]
+            xT = ps_t.tile([P, 4, P], F32)
+            for t in range(4):
+                nc.tensor.transpose(out=xT[:, t, :], in_=xs[:, P * t : P * t + P], identity=identf[:])
+            st[("xT", i)] = xT
+
+        def stage_d1(i):
+            xT = st[("xT", i)]
+            hg = h_pool.tile([P, P, 4], BF16, align_bytes=64)
+            nc.vector.tensor_tensor(
+                out=hg[:],
+                in0=xT[:].rearrange("p t r -> p r t"),
+                in1=lnw4[:].unsqueeze(1).to_broadcast([P, P, 4]),
+                op=ALU.mult,
+            )
+            st[("hg", i)] = hg
+
+        def stage_d2(i):
+            hg = st[("hg", i)]
+            hc = h_pool.tile([P, P], U32, align_bytes=64)
+            hs = h_pool.tile([P, P], U8, align_bytes=64)
+            nc.vector.quantize_mx(out=hc[:].bitcast(FP8X4), scales=hs[:], in_=hg[:].rearrange("p r t -> p (r t)"))
+            st[("hc", i)] = (hc, hs)
+
+        def stage_e(i):
+            hc, hs = st[("hc", i)]
+            psq = ps_mx.tile([P, 512], F32)
+            pskv = ps_mx.tile([P, 512], F32)
+            for c, acc in enumerate((psq, pskv)):
+                nc.tensor.matmul_mx(
+                    out=acc[:],
+                    lhsT=hc[:].bitcast(FP8X4),
+                    lhsT_scale=hs[:],
+                    rhs=wc[:, 512 * c : 512 * c + 512].bitcast(FP8X4),
+                    rhs_scale=ws[:, 512 * c : 512 * c + 512],
+                    start=True,
+                    stop=True,
+                )
+            st[("ps", i)] = (psq, pskv)
+
+        def head_cols(i, h):
+            psq, pskv = st[("ps", i)]
+            if h < 4:
+                return psq[:, HD * h : HD * h + HD]
+            return pskv[:, HD * (h - 4) : HD * (h - 4) + HD]
+
+        def stage_f(i):
+            u = i % 2
+            if u == 0:
+                o_t = o_pool.tile([P, 2, 1024], F32)
+                st[("o", i // 2)] = o_t
+            o_t = st[("o", i // 2)]
+            ssh = small.tile([P, NH], F32)
+            rh = small.tile([P, NH], F32)
+            for h in range(NH):
+                nc.scalar.activation(out=junk_h[:], in_=head_cols(i, h), func=ACT.Square, accum_out=ssh[:, h : h + 1])
+            nc.scalar.copy(out=o_t[:, u, 768:1024], in_=st[("ps", i)][1][:, 256:512])
+            nc.scalar.activation(
+                out=rh[:], in_=ssh[:], func=ACT.Abs_reciprocal_sqrt, scale=1.0 / HD, bias=eps_t[:]
+            )
+            st[("rh", i)] = rh
+
+        def stage_g(i):
+            ap, b, u = tile_coords(i)
+            a = 2 * ap + u
+            rh = st[("rh", i)]
+            t_t = t_pool.tile([P, NH, 2, HD], F32)
+            for h in range(NH):
+                qk = 0 if h < 4 else 1
+                nc.vector.scalar_tensor_tensor(
+                    out=t_t[:, h, :, :],
+                    in0=head_cols(i, h).unsqueeze(1).to_broadcast([P, 2, HD]),
+                    scalar=rh[:, h : h + 1],
+                    in1=tab[:, a, qk, :, :],
+                    op0=ALU.mult,
+                    op1=ALU.mult,
+                )
+            st[("t", i)] = t_t
+
+        def stage_h(i):
+            ap, b, u = tile_coords(i)
+            t_t = st[("t", i)]
+            o_t = st[("o", i // 2)]
+            nc.gpsimd.tensor_tensor(
+                out=o_t[:, u, 0:768].rearrange("p (h j e) -> p h j e", j=HALF, e=2),
+                in0=t_t[:, :, :, 0:HALF].rearrange("p h e j -> p h j e"),
+                in1=t_t[:, :, :, HALF:HD].rearrange("p h e j -> p h j e"),
+                op=ALU.add,
+            )
+            if u == 1:
+                sl = slice(2 * ap, 2 * ap + 2)
+                nc.sync.dma_start(out=o0v[b, :, sl, :], in_=o_t[:, :, 0:512])
+                nc.sync.dma_start(out=o1v[b, :, sl, :], in_=o_t[:, :, 512:768])
+                nc.sync.dma_start(out=o2v[b, :, sl, :], in_=o_t[:, :, 768:1024])
+
+        stages = (stage_a, stage_b, stage_c, stage_d1, stage_d2, stage_e, stage_f, stage_g, stage_h)
+        for s in range(NT + len(stages) - 1):
+            if s == 10:
+                build_tables(nc.gpsimd, 8, 16)
+            for lag, fn in enumerate(stages):
+                i = s - lag
+                if 0 <= i < NT:
+                    fn(i)

@@ -26,6 +26,21 @@ EPS = 1e-6
 NT = NB * A
 
 
+PINNED = True
+PRE = 2
+V3_G = (1, 0)
+XS_G = (0, 1)
+TAB_G = True
+
+
+def v3_on_gpsimd(i):
+    return V3_G[i % len(V3_G)] == 1
+
+
+def xs_on_gpsimd(i):
+    return XS_G[i % len(XS_G)] == 1
+
+
 def tile_qwen3block_pa_t_kernel(tc, x, ln_w, qkv_w, q_norm_w, k_norm_w, out_0, out_1, out_2):
     nc = tc.nc
     with ExitStack() as ctx:
@@ -37,6 +52,8 @@ def tile_qwen3block_pa_t_kernel(tc, x, ln_w, qkv_w, q_norm_w, k_norm_w, out_0, o
         o_pool = ctx.enter_context(tc.tile_pool(name="o_pool", bufs=3))
         ps_t = ctx.enter_context(tc.psum_pool(name="ps_t", bufs=2))
         ps_mx = ctx.enter_context(tc.psum_pool(name="ps_mx", bufs=3))
+        if PINNED:
+            ctx.enter_context(tc.manual_schedule())
 
         xv = x.rearrange("b (p a) e -> b p a e", a=A)
         o0v = out_0.rearrange("b (p a) h d -> b p a (h d)", a=A)
@@ -64,6 +81,24 @@ def tile_qwen3block_pa_t_kernel(tc, x, ln_w, qkv_w, q_norm_w, k_norm_w, out_0, o
             if g == 0:
                 nc.sync.dma_start(out=wr[:], in_=qkv_w.rearrange("(t p) n -> p t n", p=P))
 
+        ssx = const.tile([P, NT], F32)
+        rx = const.tile([P, NT], F32)
+        junk_x = const.tile([P, E], BF16)
+        junk_h = const.tile([P, HD], BF16)
+        eps_t = const.tile([P, 1], F32)
+        nc.vector.memset(eps_t[:], EPS)
+        st = {}
+
+        def stage_a1(i):
+            xt = xin[i // 2][:, i % 2, :]
+            nc.scalar.activation(out=junk_x[:], in_=xt, func=ACT.Square, accum_out=ssx[:, i : i + 1])
+
+        def stage_a2(i):
+            nc.scalar.activation(
+                out=rx[:, i : i + 1], in_=ssx[:, i : i + 1], func=ACT.Abs_reciprocal_sqrt,
+                scale=1.0 / E, bias=eps_t[:],
+            )
+
         pos_i = const.tile([P, A], I32)
         nc.gpsimd.iota(pos_i[:], pattern=[[1, A]], base=0, channel_multiplier=A)
         identf = const.tile([P, P], F32)
@@ -71,8 +106,6 @@ def tile_qwen3block_pa_t_kernel(tc, x, ln_w, qkv_w, q_norm_w, k_norm_w, out_0, o
 
         one1 = const.tile([P, 1], F32)
         nc.vector.memset(one1[:], 1.0)
-        eps_t = const.tile([P, 1], F32)
-        nc.vector.memset(eps_t[:], EPS)
         gt = const.tile([P, HALF], F32)
         nc.vector.tensor_scalar_mul(out=gt[:, 0:1], in0=one1[:], scalar1=1.0 / (2.0 * math.pi))
         n = 1
@@ -82,13 +115,17 @@ def tile_qwen3block_pa_t_kernel(tc, x, ln_w, qkv_w, q_norm_w, k_norm_w, out_0, o
         pos_f = const.tile([P, A], F32)
         nc.vector.tensor_copy(out=pos_f[:], in_=pos_i[:])
 
+        for i in range(PRE):
+            stage_a1(i)
+
         tt = const.tile([P, A, HALF], F32)
         n_s = const.tile([P, A, HALF], I32)
         f_s = const.tile([P, A, HALF], F32)
         n_c = const.tile([P, A, HALF], I32)
         f_c = const.tile([P, A, HALF], F32)
-        sin_t = const.tile([P, A, HALF], F32)
-        cos_t = const.tile([P, A, HALF], F32)
+        trig = const.tile([P, A, 3 * HALF], F32)
+        l0f = const.tile([P, P], F32)
+        xT = ps_t.tile([P, 4, P], F32)
         for a0, a1 in ((0, 8), (8, 16)):
             na = a1 - a0
             nc.vector.tensor_tensor(
@@ -104,19 +141,22 @@ def tile_qwen3block_pa_t_kernel(tc, x, ln_w, qkv_w, q_norm_w, k_norm_w, out_0, o
                 out=f_c[:, a0:a1, :], in0=tt[:, a0:a1, :], scalar=0.25, in1=n_c[:, a0:a1, :],
                 op0=ALU.add, op1=ALU.subtract,
             )
-            nc.scalar.activation(out=sin_t[:, a0:a1, :], in_=f_s[:, a0:a1, :], func=ACT.Sin, scale=2.0 * math.pi)
-            nc.scalar.activation(out=cos_t[:, a0:a1, :], in_=f_c[:, a0:a1, :], func=ACT.Sin, scale=2.0 * math.pi)
-
-        wd = const.tile([P, 2, 3, HALF], F32)
-        nc.vector.tensor_copy(out=wd[:, :, 0:2, :], in_=wn[:].rearrange("p q (j e) -> p q e j", e=2))
-        nc.vector.tensor_scalar_mul(out=wd[:, :, 2, :], in0=wd[:, :, 1, :], scalar1=-1.0)
-
-        l0f = const.tile([P, P], F32)
-        nc.vector.tensor_copy(out=l0f[:], in_=l0[:])
-        xT = ps_t.tile([P, 4, P], F32)
-        nc.tensor.transpose(out=xT[:, 0, :], in_=l0f[:], identity=identf[:])
+            nc.scalar.activation(out=trig[:, a0:a1, 0:HALF], in_=f_s[:, a0:a1, :], func=ACT.Sin, scale=2.0 * math.pi)
+            nc.scalar.activation(out=trig[:, a0:a1, 2 * HALF : 3 * HALF], in_=f_s[:, a0:a1, :], func=ACT.Sin, scale=-2.0 * math.pi)
+            nc.scalar.activation(out=trig[:, a0:a1, HALF : 2 * HALF], in_=f_c[:, a0:a1, :], func=ACT.Sin, scale=2.0 * math.pi)
+            if a0 == 0:
+                nc.vector.tensor_copy(out=l0f[:], in_=l0[:])
+                nc.tensor.transpose(out=xT[:, 0, :], in_=l0f[:], identity=identf[:])
         lnw4 = const.tile([P, 4], F32)
         nc.vector.tensor_copy(out=lnw4[:], in_=xT[:, 0, 0:4])
+
+        for i in range(PRE):
+            stage_a2(i)
+
+        wd = const.tile([P, 2, HD], F32)
+        nc.vector.tensor_copy(
+            out=wd[:].rearrange("p q (e j) -> p q e j", e=2), in_=wn[:].rearrange("p q (j e) -> p q e j", e=2)
+        )
 
         wg = const.tile([P, 1024, 4], BF16, align_bytes=64)
         wc = const.tile([P, 1024], U32, align_bytes=64)
@@ -125,57 +165,43 @@ def tile_qwen3block_pa_t_kernel(tc, x, ln_w, qkv_w, q_norm_w, k_norm_w, out_0, o
         wr_qk = wr[:, :, 0:768].rearrange("p t (h j e) -> p e h j t", e=2, j=HALF)
         for e in range(2):
             nc.gpsimd.tensor_scalar(
-                out=wg_qk[:, e, 0:4, :, :], in0=wr_qk[:, e, 0:4, :, :], scalar1=1.0, scalar2=0.0, op0=ALU.mult, op1=ALU.add
+                out=wg_qk[:, e, 0:4, :, :], in0=wr_qk[:, e, 0:4, :, :], scalar1=1.0, scalar2=0.0,
+                op0=ALU.mult, op1=ALU.add,
             )
         for e in range(2):
             nc.vector.tensor_copy(out=wg_qk[:, e, 4:6, :, :], in_=wr_qk[:, e, 4:6, :, :])
         nc.vector.tensor_copy(out=wg[:, 768:1024, :], in_=wr[:, :, 768:1024].rearrange("p t n -> p n t"))
-        for c in range(2):
+
+        tab = const.tile([P, A, 2, 2, HD], F32)
+
+        def build_tables(eng, a0, a1):
+            na = a1 - a0
+            for e_out in range(2):
+                s0 = 1 - e_out
+                eng.tensor_tensor(
+                    out=tab[:, a0:a1, :, e_out, :],
+                    in0=trig[:, a0:a1, HALF * s0 : HALF * s0 + HD].unsqueeze(2).to_broadcast([P, na, 2, HD]),
+                    in1=wd[:].unsqueeze(1).to_broadcast([P, na, 2, HD]),
+                    op=ALU.mult,
+                )
+
+        build_tables(nc.vector, 0, 2)
+        for c in (1, 0):
             nc.vector.quantize_mx(
                 out=wc[:, 512 * c : 512 * c + 512].bitcast(FP8X4),
                 scales=ws[:, 512 * c : 512 * c + 512],
                 in_=wg[:, 512 * c : 512 * c + 512, :].rearrange("p n t -> p (n t)"),
             )
 
-        tab = const.tile([P, A, 2, 2, HD], F32)
-
-        def build_tables(eng, a0, a1):
-            na = a1 - a0
-            for qk in range(2):
-                for e_out, hf, src, slot in ((0, 0, cos_t, 0), (0, 1, sin_t, 2), (1, 0, sin_t, 0), (1, 1, cos_t, 1)):
-                    eng.tensor_tensor(
-                        out=tab[:, a0:a1, qk, e_out, HALF * hf : HALF * hf + HALF],
-                        in0=src[:, a0:a1, :],
-                        in1=wd[:, qk, slot, :].unsqueeze(1).to_broadcast([P, na, HALF]),
-                        op=ALU.mult,
-                    )
-
-        build_tables(nc.vector, 0, 2)
-        build_tables(nc.gpsimd, 2, 8)
-
-        ssx = const.tile([P, NT], F32)
-        rx = const.tile([P, NT], F32)
-        junk_x = const.tile([P, E], BF16)
-        junk_h = const.tile([P, HD], BF16)
-        st = {}
-
-        def stage_a(i):
-            xt = xin[i // 2][:, i % 2, :]
-            nc.scalar.activation(out=junk_x[:], in_=xt, func=ACT.Square, accum_out=ssx[:, i : i + 1])
-            nc.scalar.activation(
-                out=rx[:, i : i + 1], in_=ssx[:, i : i + 1], func=ACT.Abs_reciprocal_sqrt,
-                scale=1.0 / E, bias=eps_t[:],
-            )
-
         def stage_b(i):
             xt = xin[i // 2][:, i % 2, :]
             xs = xs_pool.tile([P, E], F32)
-            if i % 2 == 1:
-                nc.scalar.activation(out=xs[:], in_=xt, func=ACT.Copy, scale=rx[:, i : i + 1])
-            else:
+            if xs_on_gpsimd(i):
                 nc.gpsimd.tensor_scalar(
                     out=xs[:], in0=xt, scalar1=rx[:, i : i + 1], scalar2=0.0, op0=ALU.mult, op1=ALU.add
                 )
+            else:
+                nc.scalar.activation(out=xs[:], in_=xt, func=ACT.Copy, scale=rx[:, i : i + 1])
             st[("xs", i)] = xs
 
         def stage_c(i):
@@ -225,19 +251,22 @@ def tile_qwen3block_pa_t_kernel(tc, x, ln_w, qkv_w, q_norm_w, k_norm_w, out_0, o
                 return psq[:, HD * h : HD * h + HD]
             return pskv[:, HD * (h - 4) : HD * (h - 4) + HD]
 
-        def stage_f(i):
+        def stage_f1(i):
             u = i % 2
             if u == 0:
                 o_t = o_pool.tile([P, 2, 1024], F32)
                 st[("o", i // 2)] = o_t
             o_t = st[("o", i // 2)]
             ssh = small.tile([P, NH], F32)
-            rh = small.tile([P, NH], F32)
             for h in range(NH):
                 nc.scalar.activation(out=junk_h[:], in_=head_cols(i, h), func=ACT.Square, accum_out=ssh[:, h : h + 1])
             nc.scalar.copy(out=o_t[:, u, 768:1024], in_=st[("ps", i)][1][:, 256:512])
+            st[("ssh", i)] = ssh
+
+        def stage_f2(i):
+            rh = small.tile([P, NH], F32)
             nc.scalar.activation(
-                out=rh[:], in_=ssh[:], func=ACT.Abs_reciprocal_sqrt, scale=1.0 / HD, bias=eps_t[:]
+                out=rh[:], in_=st[("ssh", i)][:], func=ACT.Abs_reciprocal_sqrt, scale=1.0 / HD, bias=eps_t[:]
             )
             st[("rh", i)] = rh
 
@@ -262,7 +291,8 @@ def tile_qwen3block_pa_t_kernel(tc, x, ln_w, qkv_w, q_norm_w, k_norm_w, out_0, o
             ap, b, u = tile_coords(i)
             t_t = st[("t", i)]
             o_t = st[("o", i // 2)]
-            nc.gpsimd.tensor_tensor(
+            eng = nc.gpsimd if v3_on_gpsimd(i) else nc.vector
+            eng.tensor_tensor(
                 out=o_t[:, u, 0:768].rearrange("p (h j e) -> p h j e", j=HALF, e=2),
                 in0=t_t[:, :, :, 0:HALF].rearrange("p h e j -> p h j e"),
                 in1=t_t[:, :, :, HALF:HD].rearrange("p h e j -> p h j e"),
@@ -274,11 +304,16 @@ def tile_qwen3block_pa_t_kernel(tc, x, ln_w, qkv_w, q_norm_w, k_norm_w, out_0, o
                 nc.sync.dma_start(out=o1v[b, :, sl, :], in_=o_t[:, :, 512:768])
                 nc.sync.dma_start(out=o2v[b, :, sl, :], in_=o_t[:, :, 768:1024])
 
-        stages = (stage_a, stage_b, stage_c, stage_d1, stage_d2, stage_e, stage_f, stage_g, stage_h)
-        for s in range(NT + len(stages) - 1):
-            if s == 10:
-                build_tables(nc.gpsimd, 8, 16)
-            for lag, fn in enumerate(stages):
+        plan = (
+            (stage_f1, 6), (stage_a1, 0), (stage_f2, 6), (stage_b, 1), (stage_a2, 0),
+            (stage_e, 5), (stage_c, 2),
+            (stage_d2, 4), (stage_g, 7), (stage_d1, 3), (stage_h, 8),
+        )
+        for s in range(NT + 8):
+            if s % 4 == 2 and s // 4 + 1 < A // 2:
+                ap = s // 4 + 1
+                build_tables(nc.gpsimd if TAB_G else nc.vector, 2 * ap, 2 * ap + 2)
+            for fn, lag in plan:
                 i = s - lag
-                if 0 <= i < NT:
+                if 0 <= i < NT and not (i < PRE and lag == 0):
                     fn(i)

@@ -28,13 +28,30 @@ NT = NB * A
 
 PINNED = True
 PRE = 2
-V3_G = (1, 0)
-XS_G = (0, 1)
-TAB_G = True
+V3_G = (1,)
+XS_G = (1, 1, 0, 0)
+TAB_V = 4
+BATCH = (1, 1, 2, 4, 4, 4, 4, 4, 4, 4)
 
 
 def v3_on_gpsimd(i):
     return V3_G[i % len(V3_G)] == 1
+
+
+def batch_table():
+    first, table = 0, {}
+    for k, nb in enumerate(BATCH):
+        for i in range(first, first + nb):
+            table[i] = (k, first, nb)
+        first += nb
+    assert first == NT
+    return table
+
+
+def fe_target(be):
+    if be < 4:
+        return 5 + 2 * be
+    return be + 9
 
 
 def xs_on_gpsimd(i):
@@ -48,6 +65,7 @@ def tile_qwen3block_pa_t_kernel(tc, x, ln_w, qkv_w, q_norm_w, k_norm_w, out_0, o
         small = ctx.enter_context(tc.tile_pool(name="small", bufs=4))
         xs_pool = ctx.enter_context(tc.tile_pool(name="xs_pool", bufs=3))
         h_pool = ctx.enter_context(tc.tile_pool(name="h_pool", bufs=3))
+        c_pool = ctx.enter_context(tc.tile_pool(name="c_pool", bufs=3))
         t_pool = ctx.enter_context(tc.tile_pool(name="t_pool", bufs=3))
         o_pool = ctx.enter_context(tc.tile_pool(name="o_pool", bufs=3))
         ps_t = ctx.enter_context(tc.psum_pool(name="ps_t", bufs=2))
@@ -88,6 +106,7 @@ def tile_qwen3block_pa_t_kernel(tc, x, ln_w, qkv_w, q_norm_w, k_norm_w, out_0, o
         eps_t = const.tile([P, 1], F32)
         nc.vector.memset(eps_t[:], EPS)
         st = {}
+        batches = batch_table()
 
         def stage_a1(i):
             xt = xin[i // 2][:, i % 2, :]
@@ -213,31 +232,39 @@ def tile_qwen3block_pa_t_kernel(tc, x, ln_w, qkv_w, q_norm_w, k_norm_w, out_0, o
 
         def stage_d1(i):
             xT = st[("xT", i)]
-            hg = h_pool.tile([P, P, 4], BF16, align_bytes=64)
+            k, first, nb = batches[i]
+            if i == first:
+                hg = h_pool.tile([P, nb, P, 4], BF16, align_bytes=64)
+                st[("hg", k)] = hg
+            hg = st[("hg", k)]
             nc.vector.tensor_tensor(
-                out=hg[:],
+                out=hg[:, i - first, :, :],
                 in0=xT[:].rearrange("p t r -> p r t"),
                 in1=lnw4[:].unsqueeze(1).to_broadcast([P, P, 4]),
                 op=ALU.mult,
             )
-            st[("hg", i)] = hg
 
         def stage_d2(i):
-            hg = st[("hg", i)]
-            hc = h_pool.tile([P, P], U32, align_bytes=64)
-            hs = h_pool.tile([P, P], U8, align_bytes=64)
-            nc.vector.quantize_mx(out=hc[:].bitcast(FP8X4), scales=hs[:], in_=hg[:].rearrange("p r t -> p (r t)"))
-            st[("hc", i)] = (hc, hs)
+            k, first, nb = batches[i]
+            hg = st[("hg", k)]
+            hc = c_pool.tile([P, nb * P], U32, align_bytes=64)
+            hs = c_pool.tile([P, nb * P], U8, align_bytes=64)
+            nc.vector.quantize_mx(
+                out=hc[:].bitcast(FP8X4), scales=hs[:], in_=hg[:].rearrange("p n r t -> p (n r t)")
+            )
+            st[("hc", k)] = (hc, hs)
 
         def stage_e(i):
-            hc, hs = st[("hc", i)]
+            k, first, nb = batches[i]
+            hc, hs = st[("hc", k)]
+            cols = slice(P * (i - first), P * (i - first) + P)
             psq = ps_mx.tile([P, 512], F32)
             pskv = ps_mx.tile([P, 512], F32)
             for c, acc in enumerate((psq, pskv)):
                 nc.tensor.matmul_mx(
                     out=acc[:],
-                    lhsT=hc[:].bitcast(FP8X4),
-                    lhsT_scale=hs[:],
+                    lhsT=hc[:, cols].bitcast(FP8X4),
+                    lhsT_scale=hs[:, cols],
                     rhs=wc[:, 512 * c : 512 * c + 512].bitcast(FP8X4),
                     rhs_scale=ws[:, 512 * c : 512 * c + 512],
                     start=True,
@@ -304,16 +331,37 @@ def tile_qwen3block_pa_t_kernel(tc, x, ln_w, qkv_w, q_norm_w, k_norm_w, out_0, o
                 nc.sync.dma_start(out=o1v[b, :, sl, :], in_=o_t[:, :, 512:768])
                 nc.sync.dma_start(out=o2v[b, :, sl, :], in_=o_t[:, :, 768:1024])
 
-        plan = (
-            (stage_f1, 6), (stage_a1, 0), (stage_f2, 6), (stage_b, 1), (stage_a2, 0),
-            (stage_e, 5), (stage_c, 2),
-            (stage_d2, 4), (stage_g, 7), (stage_d1, 3), (stage_h, 8),
-        )
-        for s in range(NT + 8):
-            if s % 4 == 2 and s // 4 + 1 < A // 2:
-                ap = s // 4 + 1
-                build_tables(nc.gpsimd if TAB_G else nc.vector, 2 * ap, 2 * ap + 2)
-            for fn, lag in plan:
-                i = s - lag
-                if 0 <= i < NT and not (i < PRE and lag == 0):
-                    fn(i)
+        def on(fn, i):
+            if 0 <= i < NT:
+                fn(i)
+
+        nfe = NT + 5
+        fe_done = 0
+        for be in range(NT + 4):
+            fe_list = []
+            while fe_done < min(nfe, fe_target(be)):
+                fe_list.append(fe_done)
+                fe_done += 1
+            on(stage_h, be - 3)
+            on(stage_f1, be - 1)
+            for f in fe_list:
+                if f >= PRE:
+                    on(stage_a1, f)
+            on(stage_f2, be - 1)
+            for f in fe_list:
+                on(stage_b, f - 1)
+                if f >= PRE:
+                    on(stage_a2, f)
+                on(stage_c, f - 2)
+                on(stage_d1, f - 3)
+            on(stage_g, be - 2)
+            for f in fe_list:
+                i = f - 4
+                if 0 <= i < NT and i == batches[i][1] + batches[i][2] - 1:
+                    stage_d2(i)
+            on(stage_e, be)
+            if 1 <= be + 1 < TAB_V:
+                build_tables(nc.vector, 2 * (be + 1), 2 * (be + 1) + 2)
+            if be % 4 == 0 and TAB_V <= be // 4 + 2 < A // 2:
+                ap = be // 4 + 2
+                build_tables(nc.gpsimd, 2 * ap, 2 * ap + 2)

@@ -29,7 +29,7 @@ NT = NB * A
 PINNED = True
 PRE = 2
 V3_G = (1,)
-XS_G = (1, 1, 0, 0)
+XS_G = (1, 0, 1, 0)
 TAB_V = 4
 BATCH = (1, 1, 2, 4, 4, 4, 4, 4, 4, 4)
 
@@ -48,10 +48,10 @@ def batch_table():
     return table
 
 
-def fe_target(be):
-    if be < 4:
-        return 5 + 2 * be
-    return be + 9
+def fe_target(k):
+    if k < 4:
+        return 7 + 2 * k
+    return k + 11
 
 
 def xs_on_gpsimd(i):
@@ -63,7 +63,7 @@ def tile_qwen3block_pa_t_kernel(tc, x, ln_w, qkv_w, q_norm_w, k_norm_w, out_0, o
     with ExitStack() as ctx:
         const = ctx.enter_context(tc.tile_pool(name="const", bufs=1))
         small = ctx.enter_context(tc.tile_pool(name="small", bufs=4))
-        xs_pool = ctx.enter_context(tc.tile_pool(name="xs_pool", bufs=3))
+        xs_pool = ctx.enter_context(tc.tile_pool(name="xs_pool", bufs=4))
         h_pool = ctx.enter_context(tc.tile_pool(name="h_pool", bufs=3))
         c_pool = ctx.enter_context(tc.tile_pool(name="c_pool", bufs=3))
         t_pool = ctx.enter_context(tc.tile_pool(name="t_pool", bufs=3))
@@ -139,10 +139,9 @@ def tile_qwen3block_pa_t_kernel(tc, x, ln_w, qkv_w, q_norm_w, k_norm_w, out_0, o
 
         tt = const.tile([P, A, HALF], F32)
         n_s = const.tile([P, A, HALF], I32)
-        f_s = const.tile([P, A, HALF], F32)
         n_c = const.tile([P, A, HALF], I32)
-        f_c = const.tile([P, A, HALF], F32)
-        trig = const.tile([P, A, 3 * HALF], F32)
+        fr = const.tile([P, 3, A, HALF], F32)
+        trig = const.tile([P, A, 2 * HD], F32)
         l0f = const.tile([P, P], F32)
         xT = ps_t.tile([P, 4, P], F32)
         for a0, a1 in ((0, 8), (8, 16)):
@@ -155,14 +154,19 @@ def tile_qwen3block_pa_t_kernel(tc, x, ln_w, qkv_w, q_norm_w, k_norm_w, out_0, o
             )
             nc.vector.tensor_copy(out=n_s[:, a0:a1, :], in_=tt[:, a0:a1, :])
             nc.vector.tensor_scalar_add(out=n_c[:, a0:a1, :], in0=tt[:, a0:a1, :], scalar1=0.25)
-            nc.vector.tensor_tensor(out=f_s[:, a0:a1, :], in0=tt[:, a0:a1, :], in1=n_s[:, a0:a1, :], op=ALU.subtract)
+            nc.vector.tensor_tensor(out=fr[:, 2, a0:a1, :], in0=tt[:, a0:a1, :], in1=n_s[:, a0:a1, :], op=ALU.subtract)
             nc.vector.scalar_tensor_tensor(
-                out=f_c[:, a0:a1, :], in0=tt[:, a0:a1, :], scalar=0.25, in1=n_c[:, a0:a1, :],
+                out=fr[:, 1, a0:a1, :], in0=tt[:, a0:a1, :], scalar=0.25, in1=n_c[:, a0:a1, :],
                 op0=ALU.add, op1=ALU.subtract,
             )
-            nc.scalar.activation(out=trig[:, a0:a1, 0:HALF], in_=f_s[:, a0:a1, :], func=ACT.Sin, scale=2.0 * math.pi)
-            nc.scalar.activation(out=trig[:, a0:a1, 2 * HALF : 3 * HALF], in_=f_s[:, a0:a1, :], func=ACT.Sin, scale=-2.0 * math.pi)
-            nc.scalar.activation(out=trig[:, a0:a1, HALF : 2 * HALF], in_=f_c[:, a0:a1, :], func=ACT.Sin, scale=2.0 * math.pi)
+            nc.vector.tensor_tensor(out=fr[:, 0, a0:a1, :], in0=n_s[:, a0:a1, :], in1=tt[:, a0:a1, :], op=ALU.subtract)
+            for f in range(2):
+                nc.scalar.activation(
+                    out=trig[:, a0:a1, HD * f : HD * f + HD].rearrange("p a (j e) -> p a j e", e=2),
+                    in_=fr[:, 1 - f : 3 - f, a0:a1, :].rearrange("p e a j -> p a j e"),
+                    func=ACT.Sin,
+                    scale=2.0 * math.pi,
+                )
             if a0 == 0:
                 nc.vector.tensor_copy(out=l0f[:], in_=l0[:])
                 nc.tensor.transpose(out=xT[:, 0, :], in_=l0f[:], identity=identf[:])
@@ -172,10 +176,12 @@ def tile_qwen3block_pa_t_kernel(tc, x, ln_w, qkv_w, q_norm_w, k_norm_w, out_0, o
         for i in range(PRE):
             stage_a2(i)
 
-        wd = const.tile([P, 2, HD], F32)
-        nc.vector.tensor_copy(
-            out=wd[:].rearrange("p q (e j) -> p q e j", e=2), in_=wn[:].rearrange("p q (j e) -> p q e j", e=2)
-        )
+        wdup = const.tile([P, 2, 2 * HD], F32)
+        for q in range(2):
+            nc.vector.tensor_copy(
+                out=wdup[:, q, :].rearrange("p (f j e) -> p f j e", f=2, e=2),
+                in_=wn[:, q, :].rearrange("p (j f) -> p f j", f=2).unsqueeze(3).to_broadcast([P, 2, HALF, 2]),
+            )
 
         wg = const.tile([P, 1024, 4], BF16, align_bytes=64)
         wc = const.tile([P, 1024], U32, align_bytes=64)
@@ -191,18 +197,16 @@ def tile_qwen3block_pa_t_kernel(tc, x, ln_w, qkv_w, q_norm_w, k_norm_w, out_0, o
             nc.vector.tensor_copy(out=wg_qk[:, e, 4:6, :, :], in_=wr_qk[:, e, 4:6, :, :])
         nc.vector.tensor_copy(out=wg[:, 768:1024, :], in_=wr[:, :, 768:1024].rearrange("p t n -> p n t"))
 
-        tab = const.tile([P, A, 2, 2, HD], F32)
+        tab = const.tile([P, A, 2, 2 * HD], F32)
 
         def build_tables(eng, a0, a1):
             na = a1 - a0
-            for e_out in range(2):
-                s0 = 1 - e_out
-                eng.tensor_tensor(
-                    out=tab[:, a0:a1, :, e_out, :],
-                    in0=trig[:, a0:a1, HALF * s0 : HALF * s0 + HD].unsqueeze(2).to_broadcast([P, na, 2, HD]),
-                    in1=wd[:].unsqueeze(1).to_broadcast([P, na, 2, HD]),
-                    op=ALU.mult,
-                )
+            eng.tensor_tensor(
+                out=tab[:, a0:a1, :, :],
+                in0=trig[:, a0:a1, :].unsqueeze(2).to_broadcast([P, na, 2, 2 * HD]),
+                in1=wdup[:].unsqueeze(1).to_broadcast([P, na, 2, 2 * HD]),
+                op=ALU.mult,
+            )
 
         build_tables(nc.vector, 0, 2)
         for c in (1, 0):
@@ -301,14 +305,14 @@ def tile_qwen3block_pa_t_kernel(tc, x, ln_w, qkv_w, q_norm_w, k_norm_w, out_0, o
             ap, b, u = tile_coords(i)
             a = 2 * ap + u
             rh = st[("rh", i)]
-            t_t = t_pool.tile([P, NH, 2, HD], F32)
+            t_t = t_pool.tile([P, NH, 2 * HD], F32)
             for h in range(NH):
                 qk = 0 if h < 4 else 1
                 nc.vector.scalar_tensor_tensor(
-                    out=t_t[:, h, :, :],
-                    in0=head_cols(i, h).unsqueeze(1).to_broadcast([P, 2, HD]),
+                    out=t_t[:, h, :].rearrange("p (d e) -> p d e", e=2),
+                    in0=head_cols(i, h).unsqueeze(2).to_broadcast([P, HD, 2]),
                     scalar=rh[:, h : h + 1],
-                    in1=tab[:, a, qk, :, :],
+                    in1=tab[:, a, qk, :].rearrange("p (d e) -> p d e", e=2),
                     op0=ALU.mult,
                     op1=ALU.mult,
                 )
@@ -320,9 +324,9 @@ def tile_qwen3block_pa_t_kernel(tc, x, ln_w, qkv_w, q_norm_w, k_norm_w, out_0, o
             o_t = st[("o", i // 2)]
             eng = nc.gpsimd if v3_on_gpsimd(i) else nc.vector
             eng.tensor_tensor(
-                out=o_t[:, u, 0:768].rearrange("p (h j e) -> p h j e", j=HALF, e=2),
-                in0=t_t[:, :, :, 0:HALF].rearrange("p h e j -> p h j e"),
-                in1=t_t[:, :, :, HALF:HD].rearrange("p h e j -> p h j e"),
+                out=o_t[:, u, 0:768].rearrange("p (h d) -> p h d", d=HD),
+                in0=t_t[:, :, 0:HD],
+                in1=t_t[:, :, HD : 2 * HD],
                 op=ALU.add,
             )
             if u == 1:
@@ -335,33 +339,32 @@ def tile_qwen3block_pa_t_kernel(tc, x, ln_w, qkv_w, q_norm_w, k_norm_w, out_0, o
             if 0 <= i < NT:
                 fn(i)
 
-        nfe = NT + 5
+        nfe = NT + 7
         fe_done = 0
-        for be in range(NT + 4):
+        for k in range(NT + 5):
             fe_list = []
-            while fe_done < min(nfe, fe_target(be)):
+            while fe_done < min(nfe, fe_target(k)):
                 fe_list.append(fe_done)
                 fe_done += 1
-            on(stage_h, be - 3)
-            on(stage_f1, be - 1)
+            on(stage_e, k - 1)
+            on(stage_h, k - 4)
+            on(stage_f1, k - 2)
+            on(stage_f2, k - 2)
             for f in fe_list:
                 if f >= PRE:
                     on(stage_a1, f)
-            on(stage_f2, be - 1)
+                if f - 1 >= PRE:
+                    on(stage_a2, f - 1)
+                on(stage_b, f - 2)
+                on(stage_c, f - 4)
+                on(stage_d1, f - 5)
+            on(stage_g, k - 3)
             for f in fe_list:
-                on(stage_b, f - 1)
-                if f >= PRE:
-                    on(stage_a2, f)
-                on(stage_c, f - 2)
-                on(stage_d1, f - 3)
-            on(stage_g, be - 2)
-            for f in fe_list:
-                i = f - 4
+                i = f - 6
                 if 0 <= i < NT and i == batches[i][1] + batches[i][2] - 1:
                     stage_d2(i)
-            on(stage_e, be)
-            if 1 <= be + 1 < TAB_V:
-                build_tables(nc.vector, 2 * (be + 1), 2 * (be + 1) + 2)
-            if be % 4 == 0 and TAB_V <= be // 4 + 2 < A // 2:
-                ap = be // 4 + 2
+            if 1 <= k + 1 < TAB_V:
+                build_tables(nc.vector, 2 * (k + 1), 2 * (k + 1) + 2)
+            if k % 4 == 1 and TAB_V <= k // 4 + 2 < A // 2:
+                ap = k // 4 + 2
                 build_tables(nc.gpsimd, 2 * ap, 2 * ap + 2)

@@ -66,6 +66,7 @@ def tile_qwen3block_pa_t_kernel(tc, x, ln_w, qkv_w, q_norm_w, k_norm_w, out_0, o
         xs_pool = ctx.enter_context(tc.tile_pool(name="xs_pool", bufs=4))
         h_pool = ctx.enter_context(tc.tile_pool(name="h_pool", bufs=3))
         c_pool = ctx.enter_context(tc.tile_pool(name="c_pool", bufs=3))
+        j_pool = ctx.enter_context(tc.tile_pool(name="j_pool", bufs=3))
         t_pool = ctx.enter_context(tc.tile_pool(name="t_pool", bufs=3))
         o_pool = ctx.enter_context(tc.tile_pool(name="o_pool", bufs=3))
         ps_t = ctx.enter_context(tc.psum_pool(name="ps_t", bufs=2))
@@ -101,8 +102,6 @@ def tile_qwen3block_pa_t_kernel(tc, x, ln_w, qkv_w, q_norm_w, k_norm_w, out_0, o
 
         ssx = const.tile([P, NT], F32)
         rx = const.tile([P, NT], F32)
-        junk_x = const.tile([P, E], BF16)
-        junk_h = const.tile([P, HD], BF16)
         eps_t = const.tile([P, 1], F32)
         nc.vector.memset(eps_t[:], EPS)
         st = {}
@@ -110,6 +109,7 @@ def tile_qwen3block_pa_t_kernel(tc, x, ln_w, qkv_w, q_norm_w, k_norm_w, out_0, o
 
         def stage_a1(i):
             xt = xin[i // 2][:, i % 2, :]
+            junk_x = j_pool.tile([P, E], BF16)
             nc.scalar.activation(out=junk_x[:], in_=xt, func=ACT.Square, accum_out=ssx[:, i : i + 1])
 
         def stage_a2(i):
@@ -289,8 +289,11 @@ def tile_qwen3block_pa_t_kernel(tc, x, ln_w, qkv_w, q_norm_w, k_norm_w, out_0, o
                 st[("o", i // 2)] = o_t
             o_t = st[("o", i // 2)]
             ssh = small.tile([P, NH], F32)
+            junk_h = j_pool.tile([P, NH, HD], BF16)
             for h in range(NH):
-                nc.scalar.activation(out=junk_h[:], in_=head_cols(i, h), func=ACT.Square, accum_out=ssh[:, h : h + 1])
+                nc.scalar.activation(
+                    out=junk_h[:, h, :], in_=head_cols(i, h), func=ACT.Square, accum_out=ssh[:, h : h + 1]
+                )
             nc.scalar.copy(out=o_t[:, u, 768:1024], in_=st[("ps", i)][1][:, 256:512])
             st[("ssh", i)] = ssh
 

@@ -27,15 +27,14 @@ NT = NB * A
 
 
 PINNED = True
-PRE = 2
-V3_G = (1,)
+PRE = 4
 XS_G = (1, 0, 1, 0)
 TAB_V = 4
 BATCH = (1, 1, 2, 4, 4, 4, 4, 4, 4, 4)
 
 
 def v3_on_gpsimd(i):
-    return V3_G[i % len(V3_G)] == 1
+    return i != NT - 1
 
 
 def batch_table():
@@ -68,7 +67,7 @@ def tile_qwen3block_pa_t_kernel(tc, x, ln_w, qkv_w, q_norm_w, k_norm_w, out_0, o
         c_pool = ctx.enter_context(tc.tile_pool(name="c_pool", bufs=3))
         j_pool = ctx.enter_context(tc.tile_pool(name="j_pool", bufs=3))
         t_pool = ctx.enter_context(tc.tile_pool(name="t_pool", bufs=3))
-        o_pool = ctx.enter_context(tc.tile_pool(name="o_pool", bufs=3))
+        o_pool = ctx.enter_context(tc.tile_pool(name="o_pool", bufs=4))
         ps_t = ctx.enter_context(tc.psum_pool(name="ps_t", bufs=2))
         ps_mx = ctx.enter_context(tc.psum_pool(name="ps_mx", bufs=3))
         if PINNED:
@@ -97,7 +96,7 @@ def tile_qwen3block_pa_t_kernel(tc, x, ln_w, qkv_w, q_norm_w, k_norm_w, out_0, o
             xg = const.tile([P, 2, E], BF16, name="xg%d" % g)
             nc.sync.dma_start(out=xg[:], in_=xv[b, :, 2 * ap : 2 * ap + 2, :])
             xin[g] = xg
-            if g == 0:
+            if g == 1:
                 nc.sync.dma_start(out=wr[:], in_=qkv_w.rearrange("(t p) n -> p t n", p=P))
 
         ssx = const.tile([P, NT], F32)
@@ -112,9 +111,9 @@ def tile_qwen3block_pa_t_kernel(tc, x, ln_w, qkv_w, q_norm_w, k_norm_w, out_0, o
             junk_x = j_pool.tile([P, E], BF16)
             nc.scalar.activation(out=junk_x[:], in_=xt, func=ACT.Square, accum_out=ssx[:, i : i + 1])
 
-        def stage_a2(i):
+        def stage_a2(i, n=1):
             nc.scalar.activation(
-                out=rx[:, i : i + 1], in_=ssx[:, i : i + 1], func=ACT.Abs_reciprocal_sqrt,
+                out=rx[:, i : i + n], in_=ssx[:, i : i + n], func=ACT.Abs_reciprocal_sqrt,
                 scale=1.0 / E, bias=eps_t[:],
             )
 
@@ -126,11 +125,15 @@ def tile_qwen3block_pa_t_kernel(tc, x, ln_w, qkv_w, q_norm_w, k_norm_w, out_0, o
         one1 = const.tile([P, 1], F32)
         nc.vector.memset(one1[:], 1.0)
         gt = const.tile([P, HALF], F32)
-        nc.vector.tensor_scalar_mul(out=gt[:, 0:1], in0=one1[:], scalar1=1.0 / (2.0 * math.pi))
-        n = 1
-        while n < HALF:
-            nc.vector.tensor_scalar_mul(out=gt[:, n : 2 * n], in0=gt[:, 0:n], scalar1=1000000.0 ** (-n / 64.0))
-            n *= 2
+        for j in range(4):
+            nc.vector.tensor_scalar_mul(
+                out=gt[:, j : j + 1], in0=one1[:], scalar1=1000000.0 ** (-j / 64.0) / (2.0 * math.pi)
+            )
+        for n in (4, 16):
+            for m in range(1, 4):
+                nc.vector.tensor_scalar_mul(
+                    out=gt[:, n * m : n * m + n], in0=gt[:, 0:n], scalar1=1000000.0 ** (-n * m / 64.0)
+                )
         pos_f = const.tile([P, A], F32)
         nc.vector.tensor_copy(out=pos_f[:], in_=pos_i[:])
 
@@ -173,8 +176,8 @@ def tile_qwen3block_pa_t_kernel(tc, x, ln_w, qkv_w, q_norm_w, k_norm_w, out_0, o
         lnw4 = const.tile([P, 4], F32)
         nc.vector.tensor_copy(out=lnw4[:], in_=xT[:, 0, 0:4])
 
-        for i in range(PRE):
-            stage_a2(i)
+        for i in range(0, PRE, 2):
+            stage_a2(i, 2)
 
         wdup = const.tile([P, 2, 2 * HD], F32)
         for q in range(2):
@@ -189,12 +192,7 @@ def tile_qwen3block_pa_t_kernel(tc, x, ln_w, qkv_w, q_norm_w, k_norm_w, out_0, o
         wg_qk = wg[:, 0:768, :].rearrange("p (h e j) t -> p e h j t", e=2, j=HALF)
         wr_qk = wr[:, :, 0:768].rearrange("p t (h j e) -> p e h j t", e=2, j=HALF)
         for e in range(2):
-            nc.gpsimd.tensor_scalar(
-                out=wg_qk[:, e, 0:4, :, :], in0=wr_qk[:, e, 0:4, :, :], scalar1=1.0, scalar2=0.0,
-                op0=ALU.mult, op1=ALU.add,
-            )
-        for e in range(2):
-            nc.vector.tensor_copy(out=wg_qk[:, e, 4:6, :, :], in_=wr_qk[:, e, 4:6, :, :])
+            nc.vector.tensor_copy(out=wg_qk[:, e, :, :, :], in_=wr_qk[:, e, :, :, :])
         nc.vector.tensor_copy(out=wg[:, 768:1024, :], in_=wr[:, :, 768:1024].rearrange("p t n -> p n t"))
 
         tab = const.tile([P, A, 2, 2 * HD], F32)
@@ -332,11 +330,15 @@ def tile_qwen3block_pa_t_kernel(tc, x, ln_w, qkv_w, q_norm_w, k_norm_w, out_0, o
                 in1=t_t[:, :, HD : 2 * HD],
                 op=ALU.add,
             )
-            if u == 1:
-                sl = slice(2 * ap, 2 * ap + 2)
-                nc.sync.dma_start(out=o0v[b, :, sl, :], in_=o_t[:, :, 0:512])
-                nc.sync.dma_start(out=o1v[b, :, sl, :], in_=o_t[:, :, 512:768])
-                nc.sync.dma_start(out=o2v[b, :, sl, :], in_=o_t[:, :, 768:1024])
+            if i >= NT - 2:
+                us, sl = slice(u, u + 1), slice(2 * ap + u, 2 * ap + u + 1)
+            elif u == 1:
+                us, sl = slice(0, 2), slice(2 * ap, 2 * ap + 2)
+            else:
+                return
+            nc.sync.dma_start(out=o0v[b, :, sl, :], in_=o_t[:, us, 0:512])
+            nc.sync.dma_start(out=o1v[b, :, sl, :], in_=o_t[:, us, 512:768])
+            nc.sync.dma_start(out=o2v[b, :, sl, :], in_=o_t[:, us, 768:1024])
 
         def on(fn, i):
             if 0 <= i < NT:
@@ -368,6 +370,6 @@ def tile_qwen3block_pa_t_kernel(tc, x, ln_w, qkv_w, q_norm_w, k_norm_w, out_0, o
                     stage_d2(i)
             if 1 <= k + 1 < TAB_V:
                 build_tables(nc.vector, 2 * (k + 1), 2 * (k + 1) + 2)
-            if k % 4 == 1 and TAB_V <= k // 4 + 2 < A // 2:
+            if k % 4 == 0 and TAB_V <= k // 4 + 2 < A // 2:
                 ap = k // 4 + 2
-                build_tables(nc.gpsimd, 2 * ap, 2 * ap + 2)
+                build_tables(nc.vector, 2 * ap, 2 * ap + 2)

@@ -16,45 +16,47 @@ ALU = mybir.AluOpType
 ACT = mybir.ActivationFunctionType
 
 P = 128
-NB = 2
-E = 512
+PACK = 4
+E = P * PACK
 A = 16
-NH = 6
+NT = 2 * A
 HD = 128
-HALF = 64
+PAIRS = HD // 2
+NQ = 4
+NH = 6
+QK = NH * HD
+F = 1024
+BANK = 512
 EPS = 1e-6
-NT = NB * A
+ROPE_BASE = 1000000.0
+
+QUANT_BATCH = (1, 1, 2, 4, 4, 4, 4, 4, 4, 4)
+EARLY = 4
+LAG_RSQRT = 1
+LAG_SCALE = 2
+LAG_TRANSPOSE = 4
+LAG_ROUND = 5
+LAG_QUANT = 6
+LAG_MATMUL = 1
+LAG_HEADNORM = 2
+LAG_ROTATE = 3
+LAG_SUM = 4
+LEAD = LAG_QUANT + max(QUANT_BATCH)
+TABLES_AT_START = 4
 
 
-PINNED = True
-PRE = 4
-XS_G = (1, 0, 1, 0)
-TAB_V = 4
-BATCH = (1, 1, 2, 4, 4, 4, 4, 4, 4, 4)
-
-
-def v3_on_gpsimd(i):
-    return i != NT - 1
-
-
-def batch_table():
+def quant_batches():
     first, table = 0, {}
-    for k, nb in enumerate(BATCH):
+    for qb, nb in enumerate(QUANT_BATCH):
         for i in range(first, first + nb):
-            table[i] = (k, first, nb)
+            table[i] = (qb, first, nb)
         first += nb
     assert first == NT
     return table
 
 
-def fe_target(k):
-    if k < 4:
-        return 7 + 2 * k
-    return k + 11
-
-
-def xs_on_gpsimd(i):
-    return XS_G[i % len(XS_G)] == 1
+def slots_by_step(step):
+    return min(LAG_QUANT + 1 + 2 * step, step + LEAD)
 
 
 def tile_qwen3block_pa_t_kernel(tc, x, ln_w, qkv_w, q_norm_w, k_norm_w, out_0, out_1, out_2):
@@ -70,8 +72,7 @@ def tile_qwen3block_pa_t_kernel(tc, x, ln_w, qkv_w, q_norm_w, k_norm_w, out_0, o
         o_pool = ctx.enter_context(tc.tile_pool(name="o_pool", bufs=4))
         ps_t = ctx.enter_context(tc.psum_pool(name="ps_t", bufs=2))
         ps_mx = ctx.enter_context(tc.psum_pool(name="ps_mx", bufs=3))
-        if PINNED:
-            ctx.enter_context(tc.manual_schedule())
+        ctx.enter_context(tc.manual_schedule())
 
         xv = x.rearrange("b (p a) e -> b p a e", a=A)
         o0v = out_0.rearrange("b (p a) h d -> b p a (h d)", a=A)
@@ -84,13 +85,13 @@ def tile_qwen3block_pa_t_kernel(tc, x, ln_w, qkv_w, q_norm_w, k_norm_w, out_0, o
 
         l0 = const.tile([P, P], BF16)
         nc.vector.memset(l0[:], 0.0)
-        nc.scalar.dma_start(out=l0[0:4, :], in_=ln_w.rearrange("(t c) -> t c", c=P))
+        nc.scalar.dma_start(out=l0[0:PACK, :], in_=ln_w.rearrange("(t c) -> t c", c=P))
         wn = const.tile([P, 2, HD], BF16)
         nc.scalar.dma_start(out=wn[:, 0, :], in_=q_norm_w.partition_broadcast(P))
         nc.scalar.dma_start(out=wn[:, 1, :], in_=k_norm_w.partition_broadcast(P))
 
         xin = {}
-        wr = const.tile([P, 4, 1024], BF16)
+        wr = const.tile([P, PACK, F], BF16)
         for g in range(NT // 2):
             ap, b = g // 2, g % 2
             xg = const.tile([P, 2, E], BF16, name="xg%d" % g)
@@ -104,14 +105,14 @@ def tile_qwen3block_pa_t_kernel(tc, x, ln_w, qkv_w, q_norm_w, k_norm_w, out_0, o
         eps_t = const.tile([P, 1], F32)
         nc.vector.memset(eps_t[:], EPS)
         st = {}
-        batches = batch_table()
+        batches = quant_batches()
 
-        def stage_a1(i):
+        def stage_square(i):
             xt = xin[i // 2][:, i % 2, :]
             junk_x = j_pool.tile([P, E], BF16)
             nc.scalar.activation(out=junk_x[:], in_=xt, func=ACT.Square, accum_out=ssx[:, i : i + 1])
 
-        def stage_a2(i, n=1):
+        def stage_rsqrt(i, n=1):
             nc.scalar.activation(
                 out=rx[:, i : i + n], in_=ssx[:, i : i + n], func=ACT.Abs_reciprocal_sqrt,
                 scale=1.0 / E, bias=eps_t[:],
@@ -124,35 +125,36 @@ def tile_qwen3block_pa_t_kernel(tc, x, ln_w, qkv_w, q_norm_w, k_norm_w, out_0, o
 
         one1 = const.tile([P, 1], F32)
         nc.vector.memset(one1[:], 1.0)
-        gt = const.tile([P, HALF], F32)
+        gt = const.tile([P, PAIRS], F32)
         for j in range(4):
             nc.vector.tensor_scalar_mul(
-                out=gt[:, j : j + 1], in0=one1[:], scalar1=1000000.0 ** (-j / 64.0) / (2.0 * math.pi)
+                out=gt[:, j : j + 1], in0=one1[:], scalar1=ROPE_BASE ** (-j / 64.0) / (2.0 * math.pi)
             )
-        for n in (4, 16):
+        for width in (4, 16):
             for m in range(1, 4):
                 nc.vector.tensor_scalar_mul(
-                    out=gt[:, n * m : n * m + n], in0=gt[:, 0:n], scalar1=1000000.0 ** (-n * m / 64.0)
+                    out=gt[:, width * m : width * m + width], in0=gt[:, 0:width],
+                    scalar1=ROPE_BASE ** (-width * m / 64.0),
                 )
         pos_f = const.tile([P, A], F32)
         nc.vector.tensor_copy(out=pos_f[:], in_=pos_i[:])
 
-        for i in range(PRE):
-            stage_a1(i)
+        for i in range(EARLY):
+            stage_square(i)
 
-        tt = const.tile([P, A, HALF], F32)
-        n_s = const.tile([P, A, HALF], I32)
-        n_c = const.tile([P, A, HALF], I32)
-        fr = const.tile([P, 3, A, HALF], F32)
+        tt = const.tile([P, A, PAIRS], F32)
+        n_s = const.tile([P, A, PAIRS], I32)
+        n_c = const.tile([P, A, PAIRS], I32)
+        fr = const.tile([P, 3, A, PAIRS], F32)
         trig = const.tile([P, A, 2 * HD], F32)
         l0f = const.tile([P, P], F32)
-        xT = ps_t.tile([P, 4, P], F32)
-        for a0, a1 in ((0, 8), (8, 16)):
+        xT = ps_t.tile([P, PACK, P], F32)
+        for a0, a1 in ((0, A // 2), (A // 2, A)):
             na = a1 - a0
             nc.vector.tensor_tensor(
                 out=tt[:, a0:a1, :],
-                in0=pos_f[:, a0:a1].unsqueeze(2).to_broadcast([P, na, HALF]),
-                in1=gt[:].unsqueeze(1).to_broadcast([P, na, HALF]),
+                in0=pos_f[:, a0:a1].unsqueeze(2).to_broadcast([P, na, PAIRS]),
+                in1=gt[:].unsqueeze(1).to_broadcast([P, na, PAIRS]),
                 op=ALU.mult,
             )
             nc.vector.tensor_copy(out=n_s[:, a0:a1, :], in_=tt[:, a0:a1, :])
@@ -173,51 +175,50 @@ def tile_qwen3block_pa_t_kernel(tc, x, ln_w, qkv_w, q_norm_w, k_norm_w, out_0, o
             if a0 == 0:
                 nc.vector.tensor_copy(out=l0f[:], in_=l0[:])
                 nc.tensor.transpose(out=xT[:, 0, :], in_=l0f[:], identity=identf[:])
-        lnw4 = const.tile([P, 4], F32)
-        nc.vector.tensor_copy(out=lnw4[:], in_=xT[:, 0, 0:4])
+        lnw4 = const.tile([P, PACK], F32)
+        nc.vector.tensor_copy(out=lnw4[:], in_=xT[:, 0, 0:PACK])
 
-        for i in range(0, PRE, 2):
-            stage_a2(i, 2)
+        for i in range(0, EARLY, 2):
+            stage_rsqrt(i, 2)
 
         wdup = const.tile([P, 2, 2 * HD], F32)
         for q in range(2):
             nc.vector.tensor_copy(
                 out=wdup[:, q, :].rearrange("p (f j e) -> p f j e", f=2, e=2),
-                in_=wn[:, q, :].rearrange("p (j f) -> p f j", f=2).unsqueeze(3).to_broadcast([P, 2, HALF, 2]),
+                in_=wn[:, q, :].rearrange("p (j f) -> p f j", f=2).unsqueeze(3).to_broadcast([P, 2, PAIRS, 2]),
             )
 
-        wg = const.tile([P, 1024, 4], BF16, align_bytes=64)
-        wc = const.tile([P, 1024], U32, align_bytes=64)
-        ws = const.tile([P, 1024], U8, align_bytes=64)
-        wg_qk = wg[:, 0:768, :].rearrange("p (h e j) t -> p e h j t", e=2, j=HALF)
-        wr_qk = wr[:, :, 0:768].rearrange("p t (h j e) -> p e h j t", e=2, j=HALF)
-        for e in range(2):
-            nc.vector.tensor_copy(out=wg_qk[:, e, :, :, :], in_=wr_qk[:, e, :, :, :])
-        nc.vector.tensor_copy(out=wg[:, 768:1024, :], in_=wr[:, :, 768:1024].rearrange("p t n -> p n t"))
+        wg = const.tile([P, F, PACK], BF16, align_bytes=64)
+        wc = const.tile([P, F], U32, align_bytes=64)
+        ws = const.tile([P, F], U8, align_bytes=64)
+        wg_qk = wg[:, 0:QK, :].rearrange("p (h f j) t -> p f h j t", f=2, j=PAIRS)
+        wr_qk = wr[:, :, 0:QK].rearrange("p t (h j f) -> p f h j t", f=2, j=PAIRS)
+        for f in range(2):
+            nc.vector.tensor_copy(out=wg_qk[:, f, :, :, :], in_=wr_qk[:, f, :, :, :])
+        nc.vector.tensor_copy(out=wg[:, QK:F, :], in_=wr[:, :, QK:F].rearrange("p t n -> p n t"))
 
         tab = const.tile([P, A, 2, 2 * HD], F32)
 
-        def build_tables(eng, a0, a1):
-            na = a1 - a0
-            eng.tensor_tensor(
-                out=tab[:, a0:a1, :, :],
-                in0=trig[:, a0:a1, :].unsqueeze(2).to_broadcast([P, na, 2, 2 * HD]),
-                in1=wdup[:].unsqueeze(1).to_broadcast([P, na, 2, 2 * HD]),
+        def build_tables(ap):
+            nc.vector.tensor_tensor(
+                out=tab[:, 2 * ap : 2 * ap + 2, :, :],
+                in0=trig[:, 2 * ap : 2 * ap + 2, :].unsqueeze(2).to_broadcast([P, 2, 2, 2 * HD]),
+                in1=wdup[:].unsqueeze(1).to_broadcast([P, 2, 2, 2 * HD]),
                 op=ALU.mult,
             )
 
-        build_tables(nc.vector, 0, 2)
+        build_tables(0)
         for c in (1, 0):
             nc.vector.quantize_mx(
-                out=wc[:, 512 * c : 512 * c + 512].bitcast(FP8X4),
-                scales=ws[:, 512 * c : 512 * c + 512],
-                in_=wg[:, 512 * c : 512 * c + 512, :].rearrange("p n t -> p (n t)"),
+                out=wc[:, BANK * c : BANK * c + BANK].bitcast(FP8X4),
+                scales=ws[:, BANK * c : BANK * c + BANK],
+                in_=wg[:, BANK * c : BANK * c + BANK, :].rearrange("p n t -> p (n t)"),
             )
 
-        def stage_b(i):
+        def stage_scale(i):
             xt = xin[i // 2][:, i % 2, :]
             xs = xs_pool.tile([P, E], F32)
-            if xs_on_gpsimd(i):
+            if i % 2 == 0:
                 nc.gpsimd.tensor_scalar(
                     out=xs[:], in0=xt, scalar1=rx[:, i : i + 1], scalar2=0.0, op0=ALU.mult, op1=ALU.add
                 )
@@ -225,50 +226,49 @@ def tile_qwen3block_pa_t_kernel(tc, x, ln_w, qkv_w, q_norm_w, k_norm_w, out_0, o
                 nc.scalar.activation(out=xs[:], in_=xt, func=ACT.Copy, scale=rx[:, i : i + 1])
             st[("xs", i)] = xs
 
-        def stage_c(i):
+        def stage_transpose(i):
             xs = st[("xs", i)]
-            xT = ps_t.tile([P, 4, P], F32)
-            for t in range(4):
+            xT = ps_t.tile([P, PACK, P], F32)
+            for t in range(PACK):
                 nc.tensor.transpose(out=xT[:, t, :], in_=xs[:, P * t : P * t + P], identity=identf[:])
             st[("xT", i)] = xT
 
-        def stage_d1(i):
+        def stage_round(i):
             xT = st[("xT", i)]
-            k, first, nb = batches[i]
+            qb, first, nb = batches[i]
             if i == first:
-                hg = h_pool.tile([P, nb, P, 4], BF16, align_bytes=64)
-                st[("hg", k)] = hg
-            hg = st[("hg", k)]
+                hg = h_pool.tile([P, nb, P, PACK], BF16, align_bytes=64)
+                st[("hg", qb)] = hg
+            hg = st[("hg", qb)]
             nc.vector.tensor_tensor(
                 out=hg[:, i - first, :, :],
                 in0=xT[:].rearrange("p t r -> p r t"),
-                in1=lnw4[:].unsqueeze(1).to_broadcast([P, P, 4]),
+                in1=lnw4[:].unsqueeze(1).to_broadcast([P, P, PACK]),
                 op=ALU.mult,
             )
 
-        def stage_d2(i):
-            k, first, nb = batches[i]
-            hg = st[("hg", k)]
+        def stage_quantise(qb, nb):
+            hg = st[("hg", qb)]
             hc = c_pool.tile([P, nb * P], U32, align_bytes=64)
             hs = c_pool.tile([P, nb * P], U8, align_bytes=64)
             nc.vector.quantize_mx(
                 out=hc[:].bitcast(FP8X4), scales=hs[:], in_=hg[:].rearrange("p n r t -> p (n r t)")
             )
-            st[("hc", k)] = (hc, hs)
+            st[("hc", qb)] = (hc, hs)
 
-        def stage_e(i):
-            k, first, nb = batches[i]
-            hc, hs = st[("hc", k)]
+        def stage_matmul(i):
+            qb, first, nb = batches[i]
+            hc, hs = st[("hc", qb)]
             cols = slice(P * (i - first), P * (i - first) + P)
-            psq = ps_mx.tile([P, 512], F32)
-            pskv = ps_mx.tile([P, 512], F32)
+            psq = ps_mx.tile([P, BANK], F32)
+            pskv = ps_mx.tile([P, BANK], F32)
             for c, acc in enumerate((psq, pskv)):
                 nc.tensor.matmul_mx(
                     out=acc[:],
                     lhsT=hc[:, cols].bitcast(FP8X4),
                     lhsT_scale=hs[:, cols],
-                    rhs=wc[:, 512 * c : 512 * c + 512].bitcast(FP8X4),
-                    rhs_scale=ws[:, 512 * c : 512 * c + 512],
+                    rhs=wc[:, BANK * c : BANK * c + BANK].bitcast(FP8X4),
+                    rhs_scale=ws[:, BANK * c : BANK * c + BANK],
                     start=True,
                     stop=True,
                 )
@@ -276,14 +276,14 @@ def tile_qwen3block_pa_t_kernel(tc, x, ln_w, qkv_w, q_norm_w, k_norm_w, out_0, o
 
         def head_cols(i, h):
             psq, pskv = st[("ps", i)]
-            if h < 4:
+            if h < NQ:
                 return psq[:, HD * h : HD * h + HD]
-            return pskv[:, HD * (h - 4) : HD * (h - 4) + HD]
+            return pskv[:, HD * (h - NQ) : HD * (h - NQ) + HD]
 
-        def stage_f1(i):
+        def stage_headnorm(i):
             u = i % 2
             if u == 0:
-                o_t = o_pool.tile([P, 2, 1024], F32)
+                o_t = o_pool.tile([P, 2, F], F32)
                 st[("o", i // 2)] = o_t
             o_t = st[("o", i // 2)]
             ssh = small.tile([P, NH], F32)
@@ -292,40 +292,35 @@ def tile_qwen3block_pa_t_kernel(tc, x, ln_w, qkv_w, q_norm_w, k_norm_w, out_0, o
                 nc.scalar.activation(
                     out=junk_h[:, h, :], in_=head_cols(i, h), func=ACT.Square, accum_out=ssh[:, h : h + 1]
                 )
-            nc.scalar.copy(out=o_t[:, u, 768:1024], in_=st[("ps", i)][1][:, 256:512])
-            st[("ssh", i)] = ssh
-
-        def stage_f2(i):
+            nc.scalar.copy(out=o_t[:, u, QK:F], in_=st[("ps", i)][1][:, BANK - (F - QK) : BANK])
             rh = small.tile([P, NH], F32)
             nc.scalar.activation(
-                out=rh[:], in_=st[("ssh", i)][:], func=ACT.Abs_reciprocal_sqrt, scale=1.0 / HD, bias=eps_t[:]
+                out=rh[:], in_=ssh[:], func=ACT.Abs_reciprocal_sqrt, scale=1.0 / HD, bias=eps_t[:]
             )
             st[("rh", i)] = rh
 
-        def stage_g(i):
+        def stage_rotate(i):
             ap, b, u = tile_coords(i)
-            a = 2 * ap + u
             rh = st[("rh", i)]
             t_t = t_pool.tile([P, NH, 2 * HD], F32)
             for h in range(NH):
-                qk = 0 if h < 4 else 1
                 nc.vector.scalar_tensor_tensor(
                     out=t_t[:, h, :].rearrange("p (d e) -> p d e", e=2),
                     in0=head_cols(i, h).unsqueeze(2).to_broadcast([P, HD, 2]),
                     scalar=rh[:, h : h + 1],
-                    in1=tab[:, a, qk, :].rearrange("p (d e) -> p d e", e=2),
+                    in1=tab[:, 2 * ap + u, 0 if h < NQ else 1, :].rearrange("p (d e) -> p d e", e=2),
                     op0=ALU.mult,
                     op1=ALU.mult,
                 )
             st[("t", i)] = t_t
 
-        def stage_h(i):
+        def stage_sum(i):
             ap, b, u = tile_coords(i)
             t_t = st[("t", i)]
             o_t = st[("o", i // 2)]
-            eng = nc.gpsimd if v3_on_gpsimd(i) else nc.vector
+            eng = nc.vector if i == NT - 1 else nc.gpsimd
             eng.tensor_tensor(
-                out=o_t[:, u, 0:768].rearrange("p (h d) -> p h d", d=HD),
+                out=o_t[:, u, 0:QK].rearrange("p (h d) -> p h d", d=HD),
                 in0=t_t[:, :, 0:HD],
                 in1=t_t[:, :, HD : 2 * HD],
                 op=ALU.add,
@@ -336,40 +331,36 @@ def tile_qwen3block_pa_t_kernel(tc, x, ln_w, qkv_w, q_norm_w, k_norm_w, out_0, o
                 us, sl = slice(0, 2), slice(2 * ap, 2 * ap + 2)
             else:
                 return
-            nc.sync.dma_start(out=o0v[b, :, sl, :], in_=o_t[:, us, 0:512])
-            nc.sync.dma_start(out=o1v[b, :, sl, :], in_=o_t[:, us, 512:768])
-            nc.sync.dma_start(out=o2v[b, :, sl, :], in_=o_t[:, us, 768:1024])
+            nc.sync.dma_start(out=o0v[b, :, sl, :], in_=o_t[:, us, 0 : NQ * HD])
+            nc.sync.dma_start(out=o1v[b, :, sl, :], in_=o_t[:, us, NQ * HD : QK])
+            nc.sync.dma_start(out=o2v[b, :, sl, :], in_=o_t[:, us, QK:F])
 
-        def on(fn, i):
+        def on(stage, i):
             if 0 <= i < NT:
-                fn(i)
+                stage(i)
 
-        nfe = NT + 7
-        fe_done = 0
-        for k in range(NT + 5):
-            fe_list = []
-            while fe_done < min(nfe, fe_target(k)):
-                fe_list.append(fe_done)
-                fe_done += 1
-            on(stage_e, k - 1)
-            on(stage_h, k - 4)
-            on(stage_f1, k - 2)
-            on(stage_f2, k - 2)
-            for f in fe_list:
-                if f >= PRE:
-                    on(stage_a1, f)
-                if f - 1 >= PRE:
-                    on(stage_a2, f - 1)
-                on(stage_b, f - 2)
-                on(stage_c, f - 4)
-                on(stage_d1, f - 5)
-            on(stage_g, k - 3)
-            for f in fe_list:
-                i = f - 6
+        slots = NT + LAG_QUANT + 1
+        written = 0
+        for step in range(NT + LAG_SUM + 1):
+            due = range(written, min(slots, slots_by_step(step)))
+            written = max(written, min(slots, slots_by_step(step)))
+            on(stage_matmul, step - LAG_MATMUL)
+            on(stage_sum, step - LAG_SUM)
+            on(stage_headnorm, step - LAG_HEADNORM)
+            for s in due:
+                if s >= EARLY:
+                    on(stage_square, s)
+                if s - LAG_RSQRT >= EARLY:
+                    on(stage_rsqrt, s - LAG_RSQRT)
+                on(stage_scale, s - LAG_SCALE)
+                on(stage_transpose, s - LAG_TRANSPOSE)
+                on(stage_round, s - LAG_ROUND)
+            on(stage_rotate, step - LAG_ROTATE)
+            for s in due:
+                i = s - LAG_QUANT
                 if 0 <= i < NT and i == batches[i][1] + batches[i][2] - 1:
-                    stage_d2(i)
-            if 1 <= k + 1 < TAB_V:
-                build_tables(nc.vector, 2 * (k + 1), 2 * (k + 1) + 2)
-            if k % 4 == 0 and TAB_V <= k // 4 + 2 < A // 2:
-                ap = k // 4 + 2
-                build_tables(nc.vector, 2 * ap, 2 * ap + 2)
+                    stage_quantise(batches[i][0], batches[i][2])
+            if step + 1 < TABLES_AT_START:
+                build_tables(step + 1)
+            elif step % 4 == 0 and TABLES_AT_START <= step // 4 + 2 < A // 2:
+                build_tables(step // 4 + 2)

@@ -86,12 +86,10 @@ def tile_qwen3block_pa_t_kernel(tc, x, ln_w, qkv_w, q_norm_w, k_norm_w, out_0, o
         l0 = const.tile([P, P], BF16)
         nc.vector.memset(l0[:], 0.0)
         nc.scalar.dma_start(out=l0[0:PACK, :], in_=ln_w.rearrange("(t c) -> t c", c=P))
-        wn = const.tile([P, 2, HD], BF16)
-        nc.scalar.dma_start(out=wn[:, 0, :], in_=q_norm_w.partition_broadcast(P))
-        nc.scalar.dma_start(out=wn[:, 1, :], in_=k_norm_w.partition_broadcast(P))
 
         xin = {}
         wr = const.tile([P, PACK, F], BF16)
+        wn = const.tile([P, 2, HD], BF16)
         for g in range(NT // 2):
             ap, b = g // 2, g % 2
             xg = const.tile([P, 2, E], BF16, name="xg%d" % g)
@@ -99,6 +97,8 @@ def tile_qwen3block_pa_t_kernel(tc, x, ln_w, qkv_w, q_norm_w, k_norm_w, out_0, o
             xin[g] = xg
             if g == 1:
                 nc.sync.dma_start(out=wr[:], in_=qkv_w.rearrange("(t p) n -> p t n", p=P))
+                nc.sync.dma_start(out=wn[:, 0, :], in_=q_norm_w.partition_broadcast(P))
+                nc.sync.dma_start(out=wn[:, 1, :], in_=k_norm_w.partition_broadcast(P))
 
         ssx = const.tile([P, NT], F32)
         rx = const.tile([P, NT], F32)
@@ -181,13 +181,6 @@ def tile_qwen3block_pa_t_kernel(tc, x, ln_w, qkv_w, q_norm_w, k_norm_w, out_0, o
         for i in range(0, EARLY, 2):
             stage_rsqrt(i, 2)
 
-        wdup = const.tile([P, 2, 2 * HD], F32)
-        for q in range(2):
-            nc.vector.tensor_copy(
-                out=wdup[:, q, :].rearrange("p (f j e) -> p f j e", f=2, e=2),
-                in_=wn[:, q, :].rearrange("p (j f) -> p f j", f=2).unsqueeze(3).to_broadcast([P, 2, PAIRS, 2]),
-            )
-
         wg = const.tile([P, F, PACK], BF16, align_bytes=64)
         wc = const.tile([P, F], U32, align_bytes=64)
         ws = const.tile([P, F], U8, align_bytes=64)
@@ -196,6 +189,13 @@ def tile_qwen3block_pa_t_kernel(tc, x, ln_w, qkv_w, q_norm_w, k_norm_w, out_0, o
         for f in range(2):
             nc.vector.tensor_copy(out=wg_qk[:, f, :, :, :], in_=wr_qk[:, f, :, :, :])
         nc.vector.tensor_copy(out=wg[:, QK:F, :], in_=wr[:, :, QK:F].rearrange("p t n -> p n t"))
+
+        wdup = const.tile([P, 2, 2 * HD], F32)
+        for q in range(2):
+            nc.vector.tensor_copy(
+                out=wdup[:, q, :].rearrange("p (f j e) -> p f j e", f=2, e=2),
+                in_=wn[:, q, :].rearrange("p (j f) -> p f j", f=2).unsqueeze(3).to_broadcast([P, 2, PAIRS, 2]),
+            )
 
         tab = const.tile([P, A, 2, 2 * HD], F32)
 
@@ -207,13 +207,13 @@ def tile_qwen3block_pa_t_kernel(tc, x, ln_w, qkv_w, q_norm_w, k_norm_w, out_0, o
                 op=ALU.mult,
             )
 
-        build_tables(0)
         for c in (1, 0):
             nc.vector.quantize_mx(
                 out=wc[:, BANK * c : BANK * c + BANK].bitcast(FP8X4),
                 scales=ws[:, BANK * c : BANK * c + BANK],
                 in_=wg[:, BANK * c : BANK * c + BANK, :].rearrange("p n t -> p (n t)"),
             )
+        build_tables(0)
 
         def stage_scale(i):
             xt = xin[i // 2][:, i % 2, :]

import math
from contextlib import ExitStack

import concourse.mybir as mybir
from concourse.masks import make_identity

FLOPS = 2 * 4096 * 512 * 1024

F32 = mybir.dt.float32
BF16 = mybir.dt.bfloat16
I32 = mybir.dt.int32
U32 = mybir.dt.uint32
U8 = mybir.dt.uint8
FP8X4 = mybir.dt.float8_e4m3fn_x4
ALU = mybir.AluOpType
ACT = mybir.ActivationFunctionType

P = 128
PACK = 4
E = P * PACK
A = 16
NT = 2 * A
HD = 128
PAIRS = HD // 2
NQ = 4
NH = 6
QK = NH * HD
F = 1024
BANK = 512
EPS = 1e-6
ROPE_BASE = 1000000.0

QUANT_BATCH = (1, 1, 2, 4, 4, 4, 4, 4, 4, 4)
EARLY = 4
LAG_RSQRT = 1
LAG_SCALE = 2
LAG_TRANSPOSE = 4
LAG_ROUND = 5
LAG_QUANT = 6
LAG_MATMUL = 1
LAG_HEADNORM = 2
LAG_ROTATE = 3
LAG_SUM = 4
LEAD = LAG_QUANT + max(QUANT_BATCH)
TABLES_AT_START = 4


def quant_batches():
    first, table = 0, {}
    for qb, nb in enumerate(QUANT_BATCH):
        for i in range(first, first + nb):
            table[i] = (qb, first, nb)
        first += nb
    assert first == NT
    return table


def slots_by_step(step):
    return min(LAG_QUANT + 1 + 2 * step, step + LEAD)


def tile_qwen3block_pa_t_kernel(tc, x, ln_w, qkv_w, q_norm_w, k_norm_w, out_0, out_1, out_2):
    nc = tc.nc
    with ExitStack() as ctx:
        const = ctx.enter_context(tc.tile_pool(name="const", bufs=1))
        small = ctx.enter_context(tc.tile_pool(name="small", bufs=4))
        xs_pool = ctx.enter_context(tc.tile_pool(name="xs_pool", bufs=4))
        h_pool = ctx.enter_context(tc.tile_pool(name="h_pool", bufs=3))
        c_pool = ctx.enter_context(tc.tile_pool(name="c_pool", bufs=3))
        j_pool = ctx.enter_context(tc.tile_pool(name="j_pool", bufs=3))
        t_pool = ctx.enter_context(tc.tile_pool(name="t_pool", bufs=3))
        o_pool = ctx.enter_context(tc.tile_pool(name="o_pool", bufs=4))
        ps_t = ctx.enter_context(tc.psum_pool(name="ps_t", bufs=2))
        ps_mx = ctx.enter_context(tc.psum_pool(name="ps_mx", bufs=3))
        ctx.enter_context(tc.manual_schedule())

        xv = x.rearrange("b (p a) e -> b p a e", a=A)
        o0v = out_0.rearrange("b (p a) h d -> b p a (h d)", a=A)
        o1v = out_1.rearrange("b (p a) h d -> b p a (h d)", a=A)
        o2v = out_2.rearrange("b (p a) h d -> b p a (h d)", a=A)

        def tile_coords(i):
            g = i // 2
            return g // 2, g % 2, i % 2

        l0 = const.tile([P, P], BF16)
        nc.vector.memset(l0[:], 0.0)
        nc.scalar.dma_start(out=l0[0:PACK, :], in_=ln_w.rearrange("(t c) -> t c", c=P))

        xin = {}
        wr = const.tile([P, PACK, F], BF16)
        wn = const.tile([P, 2, HD], BF16)
        for g in range(NT // 2):
            ap, b = g // 2, g % 2
            xg = const.tile([P, 2, E], BF16, name="xg%d" % g)
            nc.sync.dma_start(out=xg[:], in_=xv[b, :, 2 * ap : 2 * ap + 2, :])
            xin[g] = xg
            if g == 1:
                nc.sync.dma_start(out=wr[:], in_=qkv_w.rearrange("(t p) n -> p t n", p=P))
                nc.sync.dma_start(out=wn[:, 0, :], in_=q_norm_w.partition_broadcast(P))
                nc.sync.dma_start(out=wn[:, 1, :], in_=k_norm_w.partition_broadcast(P))

        ssx = const.tile([P, NT], F32)
        rx = const.tile([P, NT], F32)
        eps_t = const.tile([P, 1], F32)
        nc.vector.memset(eps_t[:], EPS)
        st = {}
        batches = quant_batches()

        def stage_square(i):
            xt = xin[i // 2][:, i % 2, :]
            junk_x = j_pool.tile([P, E], BF16)
            nc.scalar.activation(out=junk_x[:], in_=xt, func=ACT.Square, accum_out=ssx[:, i : i + 1])

        def stage_rsqrt(i, n=1):
            nc.scalar.activation(
                out=rx[:, i : i + n], in_=ssx[:, i : i + n], func=ACT.Abs_reciprocal_sqrt,
                scale=1.0 / E, bias=eps_t[:],
            )

        pos_i = const.tile([P, A], I32)
        nc.gpsimd.iota(pos_i[:], pattern=[[1, A]], base=0, channel_multiplier=A)
        identf = const.tile([P, P], F32)
        make_identity(nc, identf[:])

        one1 = const.tile([P, 1], F32)
        nc.vector.memset(one1[:], 1.0)
        gt = const.tile([P, PAIRS], F32)
        for j in range(4):
            nc.vector.tensor_scalar_mul(
                out=gt[:, j : j + 1], in0=one1[:], scalar1=ROPE_BASE ** (-j / 64.0) / (2.0 * math.pi)
            )
        for width in (4, 16):
            for m in range(1, 4):
                nc.vector.tensor_scalar_mul(
                    out=gt[:, width * m : width * m + width], in0=gt[:, 0:width],
                    scalar1=ROPE_BASE ** (-width * m / 64.0),
                )
        pos_f = const.tile([P, A], F32)
        nc.vector.tensor_copy(out=pos_f[:], in_=pos_i[:])

        for i in range(EARLY):
            stage_square(i)

        tt = const.tile([P, A, PAIRS], F32)
        n_s = const.tile([P, A, PAIRS], I32)
        n_c = const.tile([P, A, PAIRS], I32)
        fr = const.tile([P, 3, A, PAIRS], F32)
        trig = const.tile([P, A, 2 * HD], F32)
        l0f = const.tile([P, P], F32)
        xT = ps_t.tile([P, PACK, P], F32)
        for a0, a1 in ((0, A // 2), (A // 2, A)):
            na = a1 - a0
            nc.vector.tensor_tensor(
                out=tt[:, a0:a1, :],
                in0=pos_f[:, a0:a1].unsqueeze(2).to_broadcast([P, na, PAIRS]),
                in1=gt[:].unsqueeze(1).to_broadcast([P, na, PAIRS]),
                op=ALU.mult,
            )
            nc.vector.tensor_copy(out=n_s[:, a0:a1, :], in_=tt[:, a0:a1, :])
            nc.vector.tensor_scalar_add(out=n_c[:, a0:a1, :], in0=tt[:, a0:a1, :], scalar1=0.25)
            nc.vector.tensor_tensor(out=fr[:, 2, a0:a1, :], in0=tt[:, a0:a1, :], in1=n_s[:, a0:a1, :], op=ALU.subtract)
            nc.vector.scalar_tensor_tensor(
                out=fr[:, 1, a0:a1, :], in0=tt[:, a0:a1, :], scalar=0.25, in1=n_c[:, a0:a1, :],
                op0=ALU.add, op1=ALU.subtract,
            )
            nc.vector.tensor_tensor(out=fr[:, 0, a0:a1, :], in0=n_s[:, a0:a1, :], in1=tt[:, a0:a1, :], op=ALU.subtract)
            for f in range(2):
                nc.scalar.activation(
                    out=trig[:, a0:a1, HD * f : HD * f + HD].rearrange("p a (j e) -> p a j e", e=2),
                    in_=fr[:, 1 - f : 3 - f, a0:a1, :].rearrange("p e a j -> p a j e"),
                    func=ACT.Sin,
                    scale=2.0 * math.pi,
                )
            if a0 == 0:
                nc.vector.tensor_copy(out=l0f[:], in_=l0[:])
                nc.tensor.transpose(out=xT[:, 0, :], in_=l0f[:], identity=identf[:])
        lnw4 = const.tile([P, PACK], F32)
        nc.vector.tensor_copy(out=lnw4[:], in_=xT[:, 0, 0:PACK])

        for i in range(0, EARLY, 2):
            stage_rsqrt(i, 2)

        wg = const.tile([P, F, PACK], BF16, align_bytes=64)
        wc = const.tile([P, F], U32, align_bytes=64)
        ws = const.tile([P, F], U8, align_bytes=64)
        wg_qk = wg[:, 0:QK, :].rearrange("p (h f j) t -> p f h j t", f=2, j=PAIRS)
        wr_qk = wr[:, :, 0:QK].rearrange("p t (h j f) -> p f h j t", f=2, j=PAIRS)
        for f in range(2):
            nc.vector.tensor_copy(out=wg_qk[:, f, :, :, :], in_=wr_qk[:, f, :, :, :])
        nc.vector.tensor_copy(out=wg[:, QK:F, :], in_=wr[:, :, QK:F].rearrange("p t n -> p n t"))

        wdup = const.tile([P, 2, 2 * HD], F32)
        for q in range(2):
            nc.vector.tensor_copy(
                out=wdup[:, q, :].rearrange("p (f j e) -> p f j e", f=2, e=2),
                in_=wn[:, q, :].rearrange("p (j f) -> p f j", f=2).unsqueeze(3).to_broadcast([P, 2, PAIRS, 2]),
            )

        tab = const.tile([P, A, 2, 2 * HD], F32)

        def build_tables(ap):
            nc.vector.tensor_tensor(
                out=tab[:, 2 * ap : 2 * ap + 2, :, :],
                in0=trig[:, 2 * ap : 2 * ap + 2, :].unsqueeze(2).to_broadcast([P, 2, 2, 2 * HD]),
                in1=wdup[:].unsqueeze(1).to_broadcast([P, 2, 2, 2 * HD]),
                op=ALU.mult,
            )

        for c in (1, 0):
            nc.vector.quantize_mx(
                out=wc[:, BANK * c : BANK * c + BANK].bitcast(FP8X4),
                scales=ws[:, BANK * c : BANK * c + BANK],
                in_=wg[:, BANK * c : BANK * c + BANK, :].rearrange("p n t -> p (n t)"),
            )
        build_tables(0)

        def stage_scale(i):
            xt = xin[i // 2][:, i % 2, :]
            xs = xs_pool.tile([P, E], F32)
            if i % 2 == 0:
                nc.gpsimd.tensor_scalar(
                    out=xs[:], in0=xt, scalar1=rx[:, i : i + 1], scalar2=0.0, op0=ALU.mult, op1=ALU.add
                )
            else:
                nc.scalar.activation(out=xs[:], in_=xt, func=ACT.Copy, scale=rx[:, i : i + 1])
            st[("xs", i)] = xs

        def stage_transpose(i):
            xs = st[("xs", i)]
            xT = ps_t.tile([P, PACK, P], F32)
            for t in range(PACK):
                nc.tensor.transpose(out=xT[:, t, :], in_=xs[:, P * t : P * t + P], identity=identf[:])
            st[("xT", i)] = xT

        def stage_round(i):
            xT = st[("xT", i)]
            qb, first, nb = batches[i]
            if i == first:
                hg = h_pool.tile([P, nb, P, PACK], BF16, align_bytes=64)
                st[("hg", qb)] = hg
            hg = st[("hg", qb)]
            nc.vector.tensor_tensor(
                out=hg[:, i - first, :, :],
                in0=xT[:].rearrange("p t r -> p r t"),
                in1=lnw4[:].unsqueeze(1).to_broadcast([P, P, PACK]),
                op=ALU.mult,
            )

        def stage_quantise(qb, nb):
            hg = st[("hg", qb)]
            hc = c_pool.tile([P, nb * P], U32, align_bytes=64)
            hs = c_pool.tile([P, nb * P], U8, align_bytes=64)
            nc.vector.quantize_mx(
                out=hc[:].bitcast(FP8X4), scales=hs[:], in_=hg[:].rearrange("p n r t -> p (n r t)")
            )
            st[("hc", qb)] = (hc, hs)

        def stage_matmul(i):
            qb, first, nb = batches[i]
            hc, hs = st[("hc", qb)]
            cols = slice(P * (i - first), P * (i - first) + P)
            psq = ps_mx.tile([P, BANK], F32)
            pskv = ps_mx.tile([P, BANK], F32)
            for c, acc in enumerate((psq, pskv)):
                nc.tensor.matmul_mx(
                    out=acc[:],
                    lhsT=hc[:, cols].bitcast(FP8X4),
                    lhsT_scale=hs[:, cols],
                    rhs=wc[:, BANK * c : BANK * c + BANK].bitcast(FP8X4),
                    rhs_scale=ws[:, BANK * c : BANK * c + BANK],
                    start=True,
                    stop=True,
                )
            st[("ps", i)] = (psq, pskv)

        def head_cols(i, h):
            psq, pskv = st[("ps", i)]
            if h < NQ:
                return psq[:, HD * h : HD * h + HD]
            return pskv[:, HD * (h - NQ) : HD * (h - NQ) + HD]

        def stage_headnorm(i):
            u = i % 2
            if u == 0:
                o_t = o_pool.tile([P, 2, F], F32)
                st[("o", i // 2)] = o_t
            o_t = st[("o", i // 2)]
            ssh = small.tile([P, NH], F32)
            junk_h = j_pool.tile([P, NH, HD], BF16)
            for h in range(NH):
                nc.scalar.activation(
                    out=junk_h[:, h, :], in_=head_cols(i, h), func=ACT.Square, accum_out=ssh[:, h : h + 1]
                )
            nc.scalar.copy(out=o_t[:, u, QK:F], in_=st[("ps", i)][1][:, BANK - (F - QK) : BANK])
            rh = small.tile([P, NH], F32)
            nc.scalar.activation(
                out=rh[:], in_=ssh[:], func=ACT.Abs_reciprocal_sqrt, scale=1.0 / HD, bias=eps_t[:]
            )
            st[("rh", i)] = rh

        def stage_rotate(i):
            ap, b, u = tile_coords(i)
            rh = st[("rh", i)]
            t_t = t_pool.tile([P, NH, 2 * HD], F32)
            for h in range(NH):
                nc.vector.scalar_tensor_tensor(
                    out=t_t[:, h, :].rearrange("p (d e) -> p d e", e=2),
                    in0=head_cols(i, h).unsqueeze(2).to_broadcast([P, HD, 2]),
                    scalar=rh[:, h : h + 1],
                    in1=tab[:, 2 * ap + u, 0 if h < NQ else 1, :].rearrange("p (d e) -> p d e", e=2),
                    op0=ALU.mult,
                    op1=ALU.mult,
                )
            st[("t", i)] = t_t

        def stage_sum(i):
            ap, b, u = tile_coords(i)
            t_t = st[("t", i)]
            o_t = st[("o", i // 2)]
            eng = nc.vector if i == NT - 1 else nc.gpsimd
            eng.tensor_tensor(
                out=o_t[:, u, 0:QK].rearrange("p (h d) -> p h d", d=HD),
                in0=t_t[:, :, 0:HD],
                in1=t_t[:, :, HD : 2 * HD],
                op=ALU.add,
            )
            if i >= NT - 2:
                us, sl = slice(u, u + 1), slice(2 * ap + u, 2 * ap + u + 1)
            elif u == 1:
                us, sl = slice(0, 2), slice(2 * ap, 2 * ap + 2)
            else:
                return
            nc.sync.dma_start(out=o0v[b, :, sl, :], in_=o_t[:, us, 0 : NQ * HD])
            nc.sync.dma_start(out=o1v[b, :, sl, :], in_=o_t[:, us, NQ * HD : QK])
            nc.sync.dma_start(out=o2v[b, :, sl, :], in_=o_t[:, us, QK:F])

        def on(stage, i):
            if 0 <= i < NT:
                stage(i)

        slots = NT + LAG_QUANT + 1
        written = 0
        for step in range(NT + LAG_SUM + 1):
            due = range(written, min(slots, slots_by_step(step)))
            written = max(written, min(slots, slots_by_step(step)))
            on(stage_matmul, step - LAG_MATMUL)
            on(stage_sum, step - LAG_SUM)
            on(stage_headnorm, step - LAG_HEADNORM)
            for s in due:
                if s >= EARLY:
                    on(stage_square, s)
                if s - LAG_RSQRT >= EARLY:
                    on(stage_rsqrt, s - LAG_RSQRT)
                on(stage_scale, s - LAG_SCALE)
                on(stage_transpose, s - LAG_TRANSPOSE)
                on(stage_round, s - LAG_ROUND)
            on(stage_rotate, step - LAG_ROTATE)
            for s in due:
                i = s - LAG_QUANT
                if 0 <= i < NT and i == batches[i][1] + batches[i][2] - 1:
                    stage_quantise(batches[i][0], batches[i][2])
            if step + 1 < TABLES_AT_START:
                build_tables(step + 1)
            elif step % 4 == 0 and TABLES_AT_START <= step // 4 + 2 < A // 2:
                build_tables(step // 4 + 2)
